import numpy as np
import ml_dtypes


def mxq(x, axis, fmt="e4m3"):
    dtype, down = {"e4m3": (ml_dtypes.float8_e4m3fn, 7), "e5m2": (ml_dtypes.float8_e5m2, 14)}[fmt]
    v = np.moveaxis(np.asarray(x, np.float32).astype(ml_dtypes.bfloat16).astype(np.float64), axis, -1)
    blocks = v.reshape(v.shape[:-1] + (-1, 32))
    amax = np.abs(blocks).max(-1, keepdims=True)
    byte = np.maximum(np.where(amax > 0, np.frexp(amax)[1] - 1 + 127, 0) - down, 1)
    scale = np.exp2(byte - 127.0)
    codes = (blocks / scale).astype(np.float32).astype(dtype).astype(np.float64)
    return np.moveaxis((codes * scale).reshape(v.shape), -1, axis)


WIDE = False


def mx_kscale(k):
    if not WIDE:
        return np.ones(k)
    levels = np.array([10, -10, 5, -5, 0])
    if k % 512:
        return np.exp2(np.random.permutation(np.resize(levels, k // 32))).repeat(32)
    a = np.empty((k // 512, 16))
    for p in range(k // 512):
        a[p, :8] = np.random.permutation(np.resize(levels, 8))
        for g in range(8):
            far = levels[np.abs(levels - a[p, g]) >= 10]
            a[p, g + 8] = far[np.random.randint(len(far))]
    return np.exp2(a.ravel()).repeat(32)


BF16 = ml_dtypes.bfloat16


def bf(x):
    return np.asarray(x, np.float32).astype(BF16)


def f64(x):
    return np.asarray(x).astype(np.float64)


B, IN, H, OUT, L, STEPS = 4096, 512, 512, 128, 3, 3
LN_EPS = 1e-5
TAU_EPS = 1e-6


def layer_norm(v, g, b):
    m = v.mean(-1, keepdims=True)
    var = ((v - m) ** 2).mean(-1, keepdims=True)
    return (v - m) / np.sqrt(var + LN_EPS) * g + b


def setup_inputs():
    r = mx_kscale(IN)
    s = mx_kscale(H)
    s = s / s.max()
    t = mx_kscale(H)
    liq_rms = np.sqrt(L * (L + 1) / 2.0)
    return {"liq": bf(np.random.standard_normal((B, H)) * liq_rms * s),
            "h": bf(np.random.standard_normal((B, H))),
            "x": bf(np.random.standard_normal((B, IN)) * r),
            "W_in": bf(np.random.standard_normal((H, IN)) * 0.7 / np.sqrt(IN) / r),
            "b_in": bf(np.random.standard_normal(H) * 0.3),
            "W_v": bf(np.random.standard_normal((H, H)) / np.sqrt(H) * t[:, None] / s),
            "b_v": bf(np.random.standard_normal(H) * 0.5 * t),
            "W_o": bf(np.random.standard_normal((H, H)) / np.sqrt(H) / t),
            "b_o": bf(np.random.standard_normal(H) * 0.5),
            "g_att": bf(1.0 + 0.1 * np.random.standard_normal(H)),
            "beta_att": bf(np.random.standard_normal(H) * 0.3),
            "tau": bf(0.5 + 0.5 * np.random.random(H))}


def reference(liq, h, x, W_in, b_in, W_v, b_v, W_o, b_o, g_att, beta_att, tau):
    liq, h = f64(liq), f64(h)
    xin = (mxq(f64(x), 1, "e4m3") @ mxq(f64(W_in), 1, "e4m3").T) + f64(b_in)
    v = (mxq(liq, 1, "e4m3") @ mxq(f64(W_v), 1, "e4m3").T) + f64(b_v)
    att = (mxq(v, 1, "e4m3") @ mxq(f64(W_o), 1, "e4m3").T) + f64(b_o)
    z = layer_norm(att + liq, f64(g_att), f64(beta_att))
    dh = (-h + np.tanh(z + xin)) / (f64(tau) + TAU_EPS)
    return h + dh

@@ -1,0 +1,308 @@
+from contextlib import ExitStack
+
+import concourse.mybir as mybir
+from concourse.masks import make_identity
+
+F32 = mybir.dt.float32
+BF16 = mybir.dt.bfloat16
+U32 = mybir.dt.uint32
+U8 = mybir.dt.uint8
+FP8X4 = mybir.dt.float8_e4m3fn_x4
+ALU = mybir.AluOpType
+ACT = mybir.ActivationFunctionType
+
+P = 128
+B = 4096
+H = 512
+TILES = 4
+GROUP = TILES * P
+GROUPS = B // GROUP
+LN_EPS = 1e-5
+TAU_EPS = 1e-6
+
+FLOPS = 3 * 2 * B * H * H
+
+
+def tile_advancedliquidneuralnetwork_pb_t_kernel(
+    tc, liq, h, x, W_in, b_in, W_v, b_v, W_o, b_o, g_att, beta_att, tau, out
+):
+    nc = tc.nc
+
+    def group_rows(dram, g):
+        return dram[g * GROUP : (g + 1) * GROUP, :].rearrange("(p t) f -> p t f", t=TILES)
+
+    def alternate_words(words, u):
+        return words.rearrange("r (p u) -> r u p", u=2)[:, u, :]
+
+    with ExitStack() as whole:
+        consts = whole.enter_context(tc.tile_pool(name="consts", bufs=1))
+        kept = whole.enter_context(tc.tile_pool(name="kept", bufs=1))
+        rows = whole.enter_context(tc.tile_pool(name="rows", bufs=3))
+        stage = whole.enter_context(tc.tile_pool(name="stage", bufs=2))
+        codes = whole.enter_context(tc.tile_pool(name="codes", bufs=2))
+
+        ident_f32 = consts.tile([P, P], F32)
+        make_identity(nc, ident_f32[:])
+        ident_bf16 = consts.tile([P, P], BF16)
+        make_identity(nc, ident_bf16[:])
+
+        one = consts.tile([P, 1], F32)
+        nc.vector.memset(one[:], 1.0)
+        nc.scalar.sqrt(out=one[:], in_=one[:])
+
+        def quantise_k_last(src, pick_words, words_out, scales_out, turn_ps):
+            grouped = stage.tile([P, GROUP, 2], F32, align_bytes=64)
+            for pair in range(2):
+                turned = turn_ps.tile([P, 2, 2, P], F32)
+                for i in range(2):
+                    words = src[:, 2 * pair + i, :].bitcast(F32)
+                    for u in range(2):
+                        nc.tensor.transpose(
+                            out=turned[:, i, u, :], in_=pick_words(words, u), identity=ident_f32[:]
+                        )
+                nc.scalar.copy(
+                    out=grouped[:, 2 * pair * P : 2 * (pair + 1) * P, :].rearrange(
+                        "p (i c) u -> p i c u", i=2
+                    ),
+                    in_=turned[:].rearrange("p i u c -> p i c u"),
+                )
+            nc.vector.quantize_mx(
+                out=words_out[:].bitcast(FP8X4),
+                scales=scales_out[:],
+                in_=grouped[:].rearrange("p c u -> p (c u)").bitcast(BF16),
+            )
+
+        def quantise_weight(w_rows, pick_words, words_out, scales_out, turn_ps):
+            w_sb = stage.tile([P, TILES, H], BF16)
+            nc.sync.dma_start(out=w_sb[:], in_=w_rows)
+            quantise_k_last(w_sb, pick_words, words_out, scales_out, turn_ps)
+
+        def mx_pass(acc, stationary, stationary_scales, moving, moving_scales):
+            nc.tensor.matmul_mx(
+                out=acc,
+                lhsT=stationary.bitcast(FP8X4),
+                lhsT_scale=stationary_scales,
+                rhs=moving.bitcast(FP8X4),
+                rhs_scale=moving_scales,
+                start=True,
+                stop=True,
+            )
+
+        wv_words = consts.tile([P, H], U32, align_bytes=64)
+        wv_scales = consts.tile([P, H], U8, align_bytes=64)
+        wo_words = consts.tile([P, H], U32, align_bytes=64)
+        wo_scales = consts.tile([P, H], U8, align_bytes=64)
+        win_words = consts.tile([P, H], U32, align_bytes=64)
+        win_scales = consts.tile([P, H], U8, align_bytes=64)
+
+        u_groups = []
+        neg_means = []
+        sum_sq = kept.tile([P, GROUPS * TILES], F32)
+
+        with ExitStack() as first:
+            work = first.enter_context(tc.tile_pool(name="work_a", bufs=2))
+            turn_ps = first.enter_context(tc.psum_pool(name="turn_a", bufs=2))
+            vT_ps = first.enter_context(tc.psum_pool(name="vT", bufs=3))
+            att_ps = first.enter_context(tc.psum_pool(name="att", bufs=3))
+
+            quantise_weight(
+                W_v.rearrange("(p j) k -> p j k", j=TILES), alternate_words, wv_words, wv_scales, turn_ps
+            )
+            bv_bf16 = consts.tile([P, TILES], BF16)
+            nc.sync.dma_start(out=bv_bf16[:], in_=b_v.rearrange("(p j) -> p j", j=TILES))
+            bv = consts.tile([P, TILES], F32)
+            nc.vector.tensor_copy(out=bv[:], in_=bv_bf16[:])
+            bo_all = consts.tile([P, H], BF16)
+            nc.sync.dma_start(out=bo_all[:], in_=b_o.partition_broadcast(P))
+            quantise_weight(
+                W_o.rearrange("(a p) k -> p a k", p=P), alternate_words, wo_words, wo_scales, turn_ps
+            )
+
+            for g in range(GROUPS):
+                liq_sb = rows.tile([P, TILES, H], BF16)
+                nc.sync.dma_start(out=liq_sb[:], in_=group_rows(liq, g))
+                liq_words = codes.tile([P, GROUP], U32, align_bytes=64)
+                liq_scales = codes.tile([P, GROUP], U8, align_bytes=64)
+                quantise_k_last(liq_sb, alternate_words, liq_words, liq_scales, turn_ps)
+
+                u = kept.tile([P, TILES, H], F32, name="u%d" % g)
+                u_groups.append(u)
+                for t in range(TILES):
+                    nc.gpsimd.tensor_tensor(out=u[:, t, :], in0=liq_sb[:, t, :], in1=bo_all[:], op=ALU.add)
+
+                vT = work.tile([P, TILES, GROUP], BF16)
+                for j in range(TILES):
+                    vT_acc = vT_ps.tile([P, GROUP], F32)
+                    mx_pass(
+                        vT_acc[:],
+                        wv_words[:, j * P : (j + 1) * P],
+                        wv_scales[:, j * P : (j + 1) * P],
+                        liq_words[:],
+                        liq_scales[:],
+                    )
+                    nc.scalar.activation(
+                        out=vT[:, j, :], in_=vT_acc[:], func=ACT.Identity, bias=bv[:, j : j + 1]
+                    )
+                v_grouped = work.tile([P, GROUP, TILES], BF16, align_bytes=64)
+                nc.vector.tensor_copy(
+                    out=v_grouped[:].rearrange("p (c i) j -> p c j i", i=4),
+                    in_=vT[:].rearrange("p j (c i) -> p c j i", i=4),
+                )
+                v_words = codes.tile([P, GROUP], U32, align_bytes=64)
+                v_scales = codes.tile([P, GROUP], U8, align_bytes=64)
+                nc.vector.quantize_mx(
+                    out=v_words[:].bitcast(FP8X4),
+                    scales=v_scales[:],
+                    in_=v_grouped[:].rearrange("p c j -> p (c j)"),
+                )
+
+                sum_u = work.tile([P, TILES], F32)
+                for t in range(TILES):
+                    att = att_ps.tile([P, H], F32)
+                    mx_pass(
+                        att[:],
+                        v_words[:, t * P : (t + 1) * P],
+                        v_scales[:, t * P : (t + 1) * P],
+                        wo_words[:],
+                        wo_scales[:],
+                    )
+                    nc.vector.scalar_tensor_tensor(
+                        out=u[:, t, :],
+                        in0=att[:],
+                        scalar=1.0,
+                        in1=u[:, t, :],
+                        op0=ALU.mult,
+                        op1=ALU.add,
+                        accum_out=sum_u[:, t : t + 1],
+                    )
+                neg_mean = kept.tile([P, TILES], F32, name="neg_mean%d" % g)
+                neg_means.append(neg_mean)
+                nc.vector.tensor_scalar_mul(out=neg_mean[:], in0=sum_u[:], scalar1=-1.0 / H)
+                for t in range(TILES):
+                    squares = work.tile([P, H], BF16)
+                    nc.scalar.activation(
+                        out=squares[:],
+                        in_=u[:, t, :],
+                        func=ACT.Square,
+                        bias=neg_mean[:, t : t + 1],
+                        accum_out=sum_sq[:, g * TILES + t : g * TILES + t + 1],
+                    )
+
+            quantise_weight(
+                W_in.rearrange("(a p) k -> p a k", p=P), alternate_words, win_words, win_scales, turn_ps
+            )
+            g_all = consts.tile([P, H], BF16)
+            nc.sync.dma_start(out=g_all[:], in_=g_att.partition_broadcast(P))
+            vec_rows = consts.tile([P, P], BF16)
+            nc.vector.memset(vec_rows[:], 0.0)
+            for n, vec in enumerate((b_in, beta_att, tau)):
+                nc.sync.dma_start(
+                    out=vec_rows[n * TILES : (n + 1) * TILES, :], in_=vec.rearrange("(j p) -> j p", p=P)
+                )
+            vec_ps = turn_ps.tile([P, P], BF16, tag="turned")
+            nc.tensor.transpose(out=vec_ps[:], in_=vec_rows[:], identity=ident_bf16[:])
+            vec_cols = consts.tile([P, 3 * TILES], F32)
+            nc.vector.tensor_copy(out=vec_cols[:], in_=vec_ps[:, 0 : 3 * TILES])
+            tanh_bias = consts.tile([P, TILES], F32)
+            nc.vector.tensor_add(
+                out=tanh_bias[:], in0=vec_cols[:, 0:TILES], in1=vec_cols[:, TILES : 2 * TILES]
+            )
+            gate = consts.tile([P, TILES], F32)
+            nc.vector.tensor_scalar_add(
+                out=gate[:], in0=vec_cols[:, 2 * TILES : 3 * TILES], scalar1=TAU_EPS
+            )
+            nc.vector.reciprocal(out=gate[:], in_=gate[:])
+            tau_all = consts.tile([P, H], BF16)
+            nc.sync.dma_start(out=tau_all[:], in_=tau.partition_broadcast(P))
+            keep_all = consts.tile([P, H], F32)
+            nc.vector.tensor_scalar_add(out=keep_all[:], in0=tau_all[:], scalar1=TAU_EPS)
+            nc.vector.reciprocal(out=keep_all[:], in_=keep_all[:])
+            nc.vector.tensor_scalar(
+                out=keep_all[:], in0=keep_all[:], scalar1=-1.0, scalar2=1.0, op0=ALU.mult, op1=ALU.add
+            )
+
+        rstd = kept.tile([P, GROUPS * TILES], F32)
+        nc.vector.tensor_scalar(
+            out=rstd[:], in0=sum_sq[:], scalar1=1.0 / H, scalar2=LN_EPS, op0=ALU.mult, op1=ALU.add
+        )
+        nc.scalar.sqrt(out=rstd[:], in_=rstd[:])
+        nc.vector.reciprocal(out=rstd[:], in_=rstd[:])
+
+        with ExitStack() as second:
+            work = second.enter_context(tc.tile_pool(name="work_c", bufs=2))
+            turn_ps = second.enter_context(tc.psum_pool(name="turn_c", bufs=2))
+            xin_ps = second.enter_context(tc.psum_pool(name="xin", bufs=2))
+            sT_ps = second.enter_context(tc.psum_pool(name="sT", bufs=2))
+            back_ps = second.enter_context(tc.psum_pool(name="back", bufs=2))
+
+            for g in range(GROUPS):
+                x_sb = rows.tile([P, TILES, H], BF16)
+                nc.sync.dma_start(out=x_sb[:], in_=group_rows(x, g))
+                h_sb = rows.tile([P, TILES, H], BF16)
+                nc.sync.dma_start(out=h_sb[:], in_=group_rows(h, g))
+                x_words = codes.tile([P, GROUP], U32, align_bytes=64)
+                x_scales = codes.tile([P, GROUP], U8, align_bytes=64)
+                quantise_k_last(x_sb, alternate_words, x_words, x_scales, turn_ps)
+
+                h_kept = work.tile([P, TILES, H], F32)
+                for t in range(TILES):
+                    nc.gpsimd.tensor_tensor(
+                        out=h_kept[:, t, :], in0=h_sb[:, t, :], in1=keep_all[:], op=ALU.mult
+                    )
+
+                u = u_groups[g]
+                s = work.tile([P, TILES, H], F32)
+                for t in range(TILES):
+                    xin = xin_ps.tile([P, H], F32)
+                    mx_pass(
+                        xin[:],
+                        x_words[:, t * P : (t + 1) * P],
+                        x_scales[:, t * P : (t + 1) * P],
+                        win_words[:],
+                        win_scales[:],
+                    )
+                    nc.vector.scalar_tensor_tensor(
+                        out=u[:, t, :],
+                        in0=u[:, t, :],
+                        scalar=neg_means[g][:, t : t + 1],
+                        in1=g_all[:],
+                        op0=ALU.add,
+                        op1=ALU.mult,
+                    )
+                    nc.vector.scalar_tensor_tensor(
+                        out=s[:, t, :],
+                        in0=u[:, t, :],
+                        scalar=rstd[:, g * TILES + t : g * TILES + t + 1],
+                        in1=xin[:],
+                        op0=ALU.mult,
+                        op1=ALU.add,
+                    )
+
+                tanhT = work.tile([P, TILES, GROUP], F32)
+                gatedT = work.tile([P, TILES, GROUP], F32)
+                for j in range(TILES):
+                    sT = sT_ps.tile([P, GROUP], F32)
+                    for t in range(TILES):
+                        nc.tensor.transpose(
+                            out=sT[:, t * P : (t + 1) * P],
+                            in_=s[:, t, j * P : (j + 1) * P],
+                            identity=ident_f32[:],
+                        )
+                    nc.scalar.activation(
+                        out=tanhT[:, j, :], in_=sT[:], func=ACT.Tanh, bias=tanh_bias[:, j : j + 1]
+                    )
+                    nc.scalar.activation(
+                        out=gatedT[:, j, :], in_=tanhT[:, j, :], func=ACT.Copy, scale=gate[:, j : j + 1]
+                    )
+
+                out_sb = work.tile([P, TILES, H], F32)
+                for t in range(TILES):
+                    back = back_ps.tile([P, H], F32)
+                    for j in range(TILES):
+                        nc.tensor.transpose(
+                            out=back[:, j * P : (j + 1) * P],
+                            in_=gatedT[:, j, t * P : (t + 1) * P],
+                            identity=ident_f32[:],
+                        )
+                    nc.vector.tensor_tensor(out=out_sb[:, t, :], in0=back[:], in1=h_kept[:, t, :], op=ALU.add)
+                nc.sync.dma_start(out=group_rows(out, g), in_=out_sb[:])

@@ -15,7 +15,9 @@ P = 128
 B = 4096
 H = 512
 TILES = 4
-GROUP = TILES * P
+LOAD = TILES * P
+HALF = 2
+GROUP = HALF * P
 GROUPS = B // GROUP
 LN_EPS = 1e-5
 TAU_EPS = 1e-6
@@ -28,281 +30,364 @@ def tile_advancedliquidneuralnetwork_pb_t_kernel(
 ):
     nc = tc.nc
 
-    def group_rows(dram, g):
-        return dram[g * GROUP : (g + 1) * GROUP, :].rearrange("(p t) f -> p t f", t=TILES)
+    def load_rows_view(dram, n):
+        return dram[n * LOAD : (n + 1) * LOAD, :].rearrange("(p t) f -> p t f", t=TILES)
 
-    def alternate_words(words, u):
-        return words.rearrange("r (p u) -> r u p", u=2)[:, u, :]
+    with ExitStack() as ctx:
+        consts = ctx.enter_context(tc.tile_pool(name="consts", bufs=1))
+        rows = ctx.enter_context(tc.tile_pool(name="rows", bufs=3))
+        stage = ctx.enter_context(tc.tile_pool(name="stage", bufs=3))
+        codes = ctx.enter_context(tc.tile_pool(name="codes", bufs=3))
+        work = ctx.enter_context(tc.tile_pool(name="work", bufs=2))
+        ring = ctx.enter_context(tc.tile_pool(name="ring", bufs=5))
+        small = ctx.enter_context(tc.tile_pool(name="small", bufs=6))
+        one_ps = ctx.enter_context(tc.psum_pool(name="one_ps", bufs=1))
+        u_ps = ctx.enter_context(tc.psum_pool(name="u_ps", bufs=2))
+        ctx.enter_context(tc.manual_schedule())
 
-    with ExitStack() as whole:
-        consts = whole.enter_context(tc.tile_pool(name="consts", bufs=1))
-        kept = whole.enter_context(tc.tile_pool(name="kept", bufs=1))
-        rows = whole.enter_context(tc.tile_pool(name="rows", bufs=3))
-        stage = whole.enter_context(tc.tile_pool(name="stage", bufs=2))
-        codes = whole.enter_context(tc.tile_pool(name="codes", bufs=2))
+        warm = consts.tile([P, 1], F32)
+        nc.vector.memset(warm[:], 0.0)
+        nc.scalar.activation(out=warm[:], in_=warm[:], func=ACT.Tanh)
 
-        ident_f32 = consts.tile([P, P], F32)
-        make_identity(nc, ident_f32[:])
-        ident_bf16 = consts.tile([P, P], BF16)
-        make_identity(nc, ident_bf16[:])
+        ident = consts.tile([P, P], F32)
+        make_identity(nc, ident[:])
+        minus_half = consts.tile([P, HALF], F32)
+        nc.vector.memset(minus_half[:], -0.5)
 
-        one = consts.tile([P, 1], F32)
-        nc.vector.memset(one[:], 1.0)
-        nc.scalar.sqrt(out=one[:], in_=one[:])
+        def turn_words(src, pair, words):
+            for i in range(2):
+                view = src[:, 2 * pair + i, :].bitcast(F32).rearrange("r (p u) -> r u p", u=2)
+                for u in range(2):
+                    nc.tensor.transpose(out=words[:, i, u, :], in_=view[:, u, :], identity=ident[:])
 
-        def quantise_k_last(src, pick_words, words_out, scales_out, turn_ps):
-            grouped = stage.tile([P, GROUP, 2], F32, align_bytes=64)
-            for pair in range(2):
-                turned = turn_ps.tile([P, 2, 2, P], F32)
-                for i in range(2):
-                    words = src[:, 2 * pair + i, :].bitcast(F32)
-                    for u in range(2):
-                        nc.tensor.transpose(
-                            out=turned[:, i, u, :], in_=pick_words(words, u), identity=ident_f32[:]
-                        )
-                nc.scalar.copy(
-                    out=grouped[:, 2 * pair * P : 2 * (pair + 1) * P, :].rearrange(
-                        "p (i c) u -> p i c u", i=2
-                    ),
-                    in_=turned[:].rearrange("p i u c -> p i c u"),
-                )
-            nc.vector.quantize_mx(
-                out=words_out[:].bitcast(FP8X4),
-                scales=scales_out[:],
-                in_=grouped[:].rearrange("p c u -> p (c u)").bitcast(BF16),
+        def words_out(grouped, pair, words):
+            nc.scalar.copy(
+                out=grouped[:, 2 * pair * P : 2 * (pair + 1) * P, :].rearrange("p (i c) u -> p i c u", i=2),
+                in_=words[:].rearrange("p i u c -> p i c u"),
             )
 
-        def quantise_weight(w_rows, pick_words, words_out, scales_out, turn_ps):
-            w_sb = stage.tile([P, TILES, H], BF16)
-            nc.sync.dma_start(out=w_sb[:], in_=w_rows)
-            quantise_k_last(w_sb, pick_words, words_out, scales_out, turn_ps)
+        def quantise(grouped_bf16, words, scales):
+            nc.vector.quantize_mx(out=words.bitcast(FP8X4), scales=scales, in_=grouped_bf16)
 
-        def mx_pass(acc, stationary, stationary_scales, moving, moving_scales):
+        def mx_pass(acc, stationary, moving):
             nc.tensor.matmul_mx(
                 out=acc,
-                lhsT=stationary.bitcast(FP8X4),
-                lhsT_scale=stationary_scales,
-                rhs=moving.bitcast(FP8X4),
-                rhs_scale=moving_scales,
+                lhsT=stationary[0].bitcast(FP8X4),
+                lhsT_scale=stationary[1],
+                rhs=moving[0].bitcast(FP8X4),
+                rhs_scale=moving[1],
                 start=True,
                 stop=True,
             )
 
-        wv_words = consts.tile([P, H], U32, align_bytes=64)
-        wv_scales = consts.tile([P, H], U8, align_bytes=64)
-        wo_words = consts.tile([P, H], U32, align_bytes=64)
-        wo_scales = consts.tile([P, H], U8, align_bytes=64)
-        win_words = consts.tile([P, H], U32, align_bytes=64)
-        win_scales = consts.tile([P, H], U8, align_bytes=64)
+        def quantise_weight(w_sb, name, pool, tag):
+            grouped = stage.tile([P, H, 2], F32, align_bytes=64, name="w_grouped")
+            for pair in range(2):
+                words = pool.tile([P, 2, 2, P], F32, name="words_" + tag, tag=tag)
+                turn_words(w_sb, pair, words)
+                words_out(grouped, pair, words)
+            w_words = consts.tile([P, H], U32, align_bytes=64, name=name + "_words")
+            w_scales = consts.tile([P, H], U8, align_bytes=64, name=name + "_scales")
+            quantise(grouped[:].rearrange("p c u -> p (c u)").bitcast(BF16), w_words[:], w_scales[:])
+            return w_words, w_scales
 
-        u_groups = []
-        neg_means = []
-        sum_sq = kept.tile([P, GROUPS * TILES], F32)
+        def chunk(operand, i):
+            return operand[0][:, i * P : (i + 1) * P], operand[1][:, i * P : (i + 1) * P]
 
-        with ExitStack() as first:
-            work = first.enter_context(tc.tile_pool(name="work_a", bufs=2))
-            turn_ps = first.enter_context(tc.psum_pool(name="turn_a", bufs=2))
-            vT_ps = first.enter_context(tc.psum_pool(name="vT", bufs=3))
-            att_ps = first.enter_context(tc.psum_pool(name="att", bufs=3))
+        def load_weight(w):
+            w_sb = stage.tile([P, TILES, H], BF16, name="w_sb")
+            nc.sync.dma_start(out=w_sb[:], in_=w.rearrange("(p j) k -> p j k", j=TILES))
+            return w_sb
 
-            quantise_weight(
-                W_v.rearrange("(p j) k -> p j k", j=TILES), alternate_words, wv_words, wv_scales, turn_ps
+        def load_rows(dram, g, name):
+            sb = rows.tile([P, TILES, H], BF16, name=name)
+            nc.sync.dma_start(out=sb[:], in_=load_rows_view(dram, g))
+            return sb
+
+        wv_sb = load_weight(W_v)
+        vec_bf16 = consts.tile([P, 6, 16], BF16)
+        for n, vec in enumerate((b_v, b_o, b_in, beta_att, tau, g_att)):
+            nc.scalar.dma_start(out=vec_bf16[:, n, 0:TILES], in_=vec.rearrange("(p j) -> p j", j=TILES))
+        wv = quantise_weight(wv_sb, "wv", one_ps, "words")
+        wo_sb = load_weight(W_o)
+        vec_cols = consts.tile([P, 6, TILES], F32)
+        nc.vector.tensor_copy(out=vec_cols[:], in_=vec_bf16[:, :, 0:TILES])
+        bv = vec_cols[:, 0, :]
+        bo = vec_cols[:, 1, :]
+        tanh_bias = consts.tile([P, TILES], F32)
+        nc.vector.tensor_add(out=tanh_bias[:], in0=vec_cols[:, 2, :], in1=vec_cols[:, 3, :])
+        gate = consts.tile([P, TILES], F32)
+        nc.vector.tensor_scalar_add(out=gate[:], in0=vec_cols[:, 4, :], scalar1=TAU_EPS)
+        nc.vector.reciprocal(out=gate[:], in_=gate[:])
+        keep = consts.tile([P, TILES], F32)
+        nc.vector.tensor_scalar(out=keep[:], in0=gate[:], scalar1=-1.0, scalar2=1.0, op0=ALU.mult, op1=ALU.add)
+        gain = vec_cols[:, 5, :]
+        g_all = consts.tile([P, H], F32)
+        g_ps = one_ps.tile([P, TILES, P], F32, name="g_ps", tag="back")
+        for j in range(TILES):
+            nc.tensor.transpose(
+                out=g_ps[:, j, :], in_=gain[:, j : j + 1].to_broadcast([P, P]), identity=ident[:]
             )
-            bv_bf16 = consts.tile([P, TILES], BF16)
-            nc.sync.dma_start(out=bv_bf16[:], in_=b_v.rearrange("(p j) -> p j", j=TILES))
-            bv = consts.tile([P, TILES], F32)
-            nc.vector.tensor_copy(out=bv[:], in_=bv_bf16[:])
-            bo_all = consts.tile([P, H], BF16)
-            nc.sync.dma_start(out=bo_all[:], in_=b_o.partition_broadcast(P))
-            quantise_weight(
-                W_o.rearrange("(a p) k -> p a k", p=P), alternate_words, wo_words, wo_scales, turn_ps
+        nc.vector.tensor_copy(out=g_all[:], in_=g_ps[:].rearrange("p j m -> p (j m)"))
+        keep_all = consts.tile([P, H], F32)
+        k_ps = one_ps.tile([P, TILES, P], F32, name="k_ps", tag="sT")
+        for j in range(TILES):
+            nc.tensor.transpose(
+                out=k_ps[:, j, :], in_=keep[:, j : j + 1].to_broadcast([P, P]), identity=ident[:]
             )
-
-            for g in range(GROUPS):
-                liq_sb = rows.tile([P, TILES, H], BF16)
-                nc.sync.dma_start(out=liq_sb[:], in_=group_rows(liq, g))
-                liq_words = codes.tile([P, GROUP], U32, align_bytes=64)
-                liq_scales = codes.tile([P, GROUP], U8, align_bytes=64)
-                quantise_k_last(liq_sb, alternate_words, liq_words, liq_scales, turn_ps)
-
-                u = kept.tile([P, TILES, H], F32, name="u%d" % g)
-                u_groups.append(u)
-                for t in range(TILES):
-                    nc.gpsimd.tensor_tensor(out=u[:, t, :], in0=liq_sb[:, t, :], in1=bo_all[:], op=ALU.add)
-
-                vT = work.tile([P, TILES, GROUP], BF16)
-                for j in range(TILES):
-                    vT_acc = vT_ps.tile([P, GROUP], F32)
-                    mx_pass(
-                        vT_acc[:],
-                        wv_words[:, j * P : (j + 1) * P],
-                        wv_scales[:, j * P : (j + 1) * P],
-                        liq_words[:],
-                        liq_scales[:],
-                    )
-                    nc.scalar.activation(
-                        out=vT[:, j, :], in_=vT_acc[:], func=ACT.Identity, bias=bv[:, j : j + 1]
-                    )
-                v_grouped = work.tile([P, GROUP, TILES], BF16, align_bytes=64)
-                nc.vector.tensor_copy(
-                    out=v_grouped[:].rearrange("p (c i) j -> p c j i", i=4),
-                    in_=vT[:].rearrange("p j (c i) -> p c j i", i=4),
-                )
-                v_words = codes.tile([P, GROUP], U32, align_bytes=64)
-                v_scales = codes.tile([P, GROUP], U8, align_bytes=64)
-                nc.vector.quantize_mx(
-                    out=v_words[:].bitcast(FP8X4),
-                    scales=v_scales[:],
-                    in_=v_grouped[:].rearrange("p c j -> p (c j)"),
-                )
-
-                sum_u = work.tile([P, TILES], F32)
-                for t in range(TILES):
-                    att = att_ps.tile([P, H], F32)
-                    mx_pass(
-                        att[:],
-                        v_words[:, t * P : (t + 1) * P],
-                        v_scales[:, t * P : (t + 1) * P],
-                        wo_words[:],
-                        wo_scales[:],
-                    )
-                    nc.vector.scalar_tensor_tensor(
-                        out=u[:, t, :],
-                        in0=att[:],
-                        scalar=1.0,
-                        in1=u[:, t, :],
-                        op0=ALU.mult,
-                        op1=ALU.add,
-                        accum_out=sum_u[:, t : t + 1],
-                    )
-                neg_mean = kept.tile([P, TILES], F32, name="neg_mean%d" % g)
-                neg_means.append(neg_mean)
-                nc.vector.tensor_scalar_mul(out=neg_mean[:], in0=sum_u[:], scalar1=-1.0 / H)
-                for t in range(TILES):
-                    squares = work.tile([P, H], BF16)
-                    nc.scalar.activation(
-                        out=squares[:],
-                        in_=u[:, t, :],
-                        func=ACT.Square,
-                        bias=neg_mean[:, t : t + 1],
-                        accum_out=sum_sq[:, g * TILES + t : g * TILES + t + 1],
-                    )
-
-            quantise_weight(
-                W_in.rearrange("(a p) k -> p a k", p=P), alternate_words, win_words, win_scales, turn_ps
-            )
-            g_all = consts.tile([P, H], BF16)
-            nc.sync.dma_start(out=g_all[:], in_=g_att.partition_broadcast(P))
-            vec_rows = consts.tile([P, P], BF16)
-            nc.vector.memset(vec_rows[:], 0.0)
-            for n, vec in enumerate((b_in, beta_att, tau)):
-                nc.sync.dma_start(
-                    out=vec_rows[n * TILES : (n + 1) * TILES, :], in_=vec.rearrange("(j p) -> j p", p=P)
-                )
-            vec_ps = turn_ps.tile([P, P], BF16, tag="turned")
-            nc.tensor.transpose(out=vec_ps[:], in_=vec_rows[:], identity=ident_bf16[:])
-            vec_cols = consts.tile([P, 3 * TILES], F32)
-            nc.vector.tensor_copy(out=vec_cols[:], in_=vec_ps[:, 0 : 3 * TILES])
-            tanh_bias = consts.tile([P, TILES], F32)
-            nc.vector.tensor_add(
-                out=tanh_bias[:], in0=vec_cols[:, 0:TILES], in1=vec_cols[:, TILES : 2 * TILES]
-            )
-            gate = consts.tile([P, TILES], F32)
-            nc.vector.tensor_scalar_add(
-                out=gate[:], in0=vec_cols[:, 2 * TILES : 3 * TILES], scalar1=TAU_EPS
-            )
-            nc.vector.reciprocal(out=gate[:], in_=gate[:])
-            tau_all = consts.tile([P, H], BF16)
-            nc.sync.dma_start(out=tau_all[:], in_=tau.partition_broadcast(P))
-            keep_all = consts.tile([P, H], F32)
-            nc.vector.tensor_scalar_add(out=keep_all[:], in0=tau_all[:], scalar1=TAU_EPS)
-            nc.vector.reciprocal(out=keep_all[:], in_=keep_all[:])
-            nc.vector.tensor_scalar(
-                out=keep_all[:], in0=keep_all[:], scalar1=-1.0, scalar2=1.0, op0=ALU.mult, op1=ALU.add
-            )
-
-        rstd = kept.tile([P, GROUPS * TILES], F32)
-        nc.vector.tensor_scalar(
-            out=rstd[:], in0=sum_sq[:], scalar1=1.0 / H, scalar2=LN_EPS, op0=ALU.mult, op1=ALU.add
+        nc.vector.tensor_copy(
+            out=keep_all[:].rearrange("p (m j) -> p m j", j=TILES), in_=k_ps[:].rearrange("p j m -> p m j")
         )
-        nc.scalar.sqrt(out=rstd[:], in_=rstd[:])
-        nc.vector.reciprocal(out=rstd[:], in_=rstd[:])
 
-        with ExitStack() as second:
-            work = second.enter_context(tc.tile_pool(name="work_c", bufs=2))
-            turn_ps = second.enter_context(tc.psum_pool(name="turn_c", bufs=2))
-            xin_ps = second.enter_context(tc.psum_pool(name="xin", bufs=2))
-            sT_ps = second.enter_context(tc.psum_pool(name="sT", bufs=2))
-            back_ps = second.enter_context(tc.psum_pool(name="back", bufs=2))
+        st = [{} for g in range(GROUPS)]
 
-            for g in range(GROUPS):
-                x_sb = rows.tile([P, TILES, H], BF16)
-                nc.sync.dma_start(out=x_sb[:], in_=group_rows(x, g))
-                h_sb = rows.tile([P, TILES, H], BF16)
-                nc.sync.dma_start(out=h_sb[:], in_=group_rows(h, g))
-                x_words = codes.tile([P, GROUP], U32, align_bytes=64)
-                x_scales = codes.tile([P, GROUP], U8, align_bytes=64)
-                quantise_k_last(x_sb, alternate_words, x_words, x_scales, turn_ps)
+        def codes_tile(name):
+            return (
+                codes.tile([P, GROUP], U32, align_bytes=64, name=name + "_words"),
+                codes.tile([P, GROUP], U8, align_bytes=64, name=name + "_scales"),
+            )
 
-                h_kept = work.tile([P, TILES, H], F32)
-                for t in range(TILES):
-                    nc.gpsimd.tensor_tensor(
-                        out=h_kept[:, t, :], in0=h_sb[:, t, :], in1=keep_all[:], op=ALU.mult
+        def whole(q):
+            return q[0][:], q[1][:]
+
+        def bf16_view(grouped):
+            return grouped[:].rearrange("p c u -> p (c u)").bitcast(BF16)
+
+        def words_stage(g, name):
+            s = st[g]
+            s[name + "T"] = stage.tile([P, GROUP, 2], F32, align_bytes=64, name=name + "T")
+            s["words"] = one_ps.tile([P, 2, 2, P], F32, name="words", tag="words")
+            turn_words(loaded[name, g // 2], g % 2, s["words"])
+
+        def words_copy(g, name):
+            words_out(st[g][name + "T"], 0, st[g]["words"])
+
+        def quantise_stage(g, name):
+            s = st[g]
+            s[name + "_q"] = codes_tile(name)
+            src = s["v_bf16"][:].rearrange("p n j -> p (n j)") if name == "v" else bf16_view(s[name + "T"])
+            quantise(src, *whole(s[name + "_q"]))
+
+        def v_mx(g, t):
+            s = st[g]
+            s["v_acc"] = one_ps.tile([P, TILES, P], F32, name="v_acc", tag="v_acc")
+            for j in range(TILES):
+                mx_pass(s["v_acc"][:, j, :], chunk(wv, j), chunk(s["liq_q"], t))
+
+        def v_out(g, t):
+            s = st[g]
+            if t == 0:
+                s["v_bf16"] = stage.tile([P, GROUP, TILES], BF16, align_bytes=64, name="v_bf16")
+            nc.vector.tensor_tensor(
+                out=s["v_bf16"][:, t * P : (t + 1) * P, :],
+                in0=s["v_acc"][:].rearrange("p j n -> p n j"),
+                in1=bv.unsqueeze(1).to_broadcast([P, P, TILES]),
+                op=ALU.add,
+            )
+
+        def att_mx(g, i):
+            s = st[g]
+            s["att"] = one_ps.tile([P, 2, GROUP], F32, name="att", tag="att")
+            for jj in range(2):
+                mx_pass(s["att"][:, jj, :], chunk(wo, 2 * i + jj), whole(s["v_q"]))
+
+        def uT_out(g, i):
+            s = st[g]
+            if i == 0:
+                s["uT"] = work.tile([P, TILES, GROUP], F32, name="uT")
+            for jj in range(2):
+                j = 2 * i + jj
+                nc.vector.scalar_tensor_tensor(
+                    out=s["uT"][:, j, :],
+                    in0=s["att"][:, jj, :],
+                    scalar=bo[:, j : j + 1],
+                    in1=bf16_view(s["liqT"]).rearrange("p (n j) -> p j n", j=TILES)[:, j, :],
+                    op0=ALU.add,
+                    op1=ALU.add,
+                )
+
+        def u_turn(g, t):
+            s = st[g]
+            u_acc = u_ps.tile([P, TILES, P], F32, name="u_acc", tag="u_acc")
+            for j in range(TILES):
+                nc.tensor.transpose(
+                    out=u_acc[:, j, :], in_=s["uT"][:, j, t * P : (t + 1) * P], identity=ident[:]
+                )
+            s["u", t] = u_acc[:].rearrange("p j m -> p (j m)")
+
+        def stats(g, t):
+            s = st[g]
+            s["neg_mean", t] = small.tile([P, 1], F32, name="neg_mean")
+            unused = work.tile([P, H], BF16, name="unused")
+            nc.scalar.activation(
+                out=unused[:], in_=s["u", t], func=ACT.Copy, scale=-1.0 / H, accum_out=s["neg_mean", t][:]
+            )
+
+        def squares(g, t):
+            s = st[g]
+            if t == 0:
+                s["sum_sq"] = small.tile([P, HALF], F32, name="sum_sq")
+            unused = work.tile([P, H], BF16, name="unused")
+            nc.scalar.activation(
+                out=unused[:],
+                in_=s["u", t],
+                func=ACT.Square,
+                bias=s["neg_mean", t][:],
+                accum_out=s["sum_sq"][:, t : t + 1],
+            )
+
+        def rstd_stage(g):
+            s = st[g]
+            r = small.tile([P, HALF], F32, name="rstd")
+            s["rstd"] = r
+            nc.gpsimd.tensor_scalar(
+                out=r[:], in0=s["sum_sq"][:], scalar1=1.0 / H, scalar2=LN_EPS,
+                op0=ALU.mult, op1=ALU.add,
+            )
+            nc.gpsimd.tensor_tensor(out=r[:], in0=r[:], in1=minus_half[:], op=ALU.pow)
+
+        def w_out(g, t):
+            s = st[g]
+            s["w", t] = ring.tile([P, H], F32, name="w")
+            nc.vector.scalar_tensor_tensor(
+                out=s["w", t][:], in0=s["u", t], scalar=s["neg_mean", t][:], in1=g_all[:],
+                op0=ALU.add, op1=ALU.mult,
+            )
+
+        def xin_mx(g, t):
+            s = st[g]
+            s["xin"] = one_ps.tile([P, H], F32, name="xin", tag="xin")
+            mx_pass(s["xin"][:], chunk(s["x_q"], t), win_q)
+
+        def s_out(g, t):
+            s = st[g]
+            if t == 0:
+                s["s"] = work.tile([P, HALF, H], F32, name="s")
+            nc.vector.scalar_tensor_tensor(
+                out=s["s"][:, t, :], in0=s["w", t][:], scalar=s["rstd"][:, t : t + 1],
+                in1=s["xin"][:], op0=ALU.mult, op1=ALU.add,
+            )
+
+        def s_turn(g, i):
+            s = st[g]
+            s["sT"] = one_ps.tile([P, 2, HALF, P], F32, name="sT", tag="sT")
+            for jj in range(2):
+                j = 2 * i + jj
+                for t in range(HALF):
+                    nc.tensor.transpose(
+                        out=s["sT"][:, jj, t, :], in_=s["s"][:, t, j * P : (j + 1) * P], identity=ident[:]
                     )
 
-                u = u_groups[g]
-                s = work.tile([P, TILES, H], F32)
-                for t in range(TILES):
-                    xin = xin_ps.tile([P, H], F32)
-                    mx_pass(
-                        xin[:],
-                        x_words[:, t * P : (t + 1) * P],
-                        x_scales[:, t * P : (t + 1) * P],
-                        win_words[:],
-                        win_scales[:],
-                    )
-                    nc.vector.scalar_tensor_tensor(
-                        out=u[:, t, :],
-                        in0=u[:, t, :],
-                        scalar=neg_means[g][:, t : t + 1],
-                        in1=g_all[:],
-                        op0=ALU.add,
-                        op1=ALU.mult,
-                    )
-                    nc.vector.scalar_tensor_tensor(
-                        out=s[:, t, :],
-                        in0=u[:, t, :],
-                        scalar=rstd[:, g * TILES + t : g * TILES + t + 1],
-                        in1=xin[:],
-                        op0=ALU.mult,
-                        op1=ALU.add,
-                    )
+        def tanh_stage(g, i):
+            s = st[g]
+            if i == 0:
+                s["gatedT"] = work.tile([P, TILES, GROUP], F32, name="gatedT")
+            tanhT = work.tile([P, 2, GROUP], F32, name="tanhT")
+            for jj in range(2):
+                j = 2 * i + jj
+                nc.scalar.activation(
+                    out=tanhT[:, jj, :], in_=s["sT"][:, jj, :, :].rearrange("p t n -> p (t n)"), func=ACT.Tanh,
+                    bias=tanh_bias[:, j : j + 1],
+                )
+            for jj in range(2):
+                j = 2 * i + jj
+                nc.scalar.activation(
+                    out=s["gatedT"][:, j, :], in_=tanhT[:, jj, :], func=ACT.Copy, scale=gate[:, j : j + 1]
+                )
 
-                tanhT = work.tile([P, TILES, GROUP], F32)
-                gatedT = work.tile([P, TILES, GROUP], F32)
-                for j in range(TILES):
-                    sT = sT_ps.tile([P, GROUP], F32)
-                    for t in range(TILES):
-                        nc.tensor.transpose(
-                            out=sT[:, t * P : (t + 1) * P],
-                            in_=s[:, t, j * P : (j + 1) * P],
-                            identity=ident_f32[:],
-                        )
-                    nc.scalar.activation(
-                        out=tanhT[:, j, :], in_=sT[:], func=ACT.Tanh, bias=tanh_bias[:, j : j + 1]
-                    )
-                    nc.scalar.activation(
-                        out=gatedT[:, j, :], in_=tanhT[:, j, :], func=ACT.Copy, scale=gate[:, j : j + 1]
-                    )
+        def keep_stage(g, t):
+            s = st[g]
+            s["h_kept", t] = ring.tile([P, H], F32, name="h_kept")
+            nc.gpsimd.tensor_tensor(
+                out=s["h_kept", t][:], in0=loaded["h", g // 2][:, 2 * (g % 2) + t, :], in1=keep_all[:], op=ALU.mult
+            )
 
-                out_sb = work.tile([P, TILES, H], F32)
-                for t in range(TILES):
-                    back = back_ps.tile([P, H], F32)
-                    for j in range(TILES):
-                        nc.tensor.transpose(
-                            out=back[:, j * P : (j + 1) * P],
-                            in_=gatedT[:, j, t * P : (t + 1) * P],
-                            identity=ident_f32[:],
-                        )
-                    nc.vector.tensor_tensor(out=out_sb[:, t, :], in0=back[:], in1=h_kept[:, t, :], op=ALU.add)
-                nc.sync.dma_start(out=group_rows(out, g), in_=out_sb[:])
+        def back_turn(g, t):
+            s = st[g]
+            s["back"] = one_ps.tile([P, TILES, P], F32, name="back", tag="back")
+            for j in range(TILES):
+                nc.tensor.transpose(
+                    out=s["back"][:, j, :], in_=s["gatedT"][:, j, t * P : (t + 1) * P], identity=ident[:]
+                )
+
+        def out_stage(g, t):
+            s = st[g]
+            if t == 0:
+                s["out"] = work.tile([P, HALF, H], F32, name="out_sb")
+            nc.vector.tensor_tensor(
+                out=s["out"][:, t, :].rearrange("p (m j) -> p m j", j=TILES),
+                in0=s["back"][:].rearrange("p j m -> p m j"),
+                in1=s["h_kept", t][:].rearrange("p (m j) -> p m j", j=TILES),
+                op=ALU.add,
+            )
+            if t == HALF - 1:
+                first = 2 * (g % 2)
+                nc.sync.dma_start(
+                    out=load_rows_view(out, g // 2)[:, first : first + HALF, :], in_=s["out"][:]
+                )
+
+        X0 = 4
+        V0, ATT0, U0, S0, T0, B0 = 2, 4, 6, 8, 10, 13
+
+        def item(k, first):
+            n = k - first
+            return divmod(n, HALF) if 0 <= n < GROUPS * HALF else None
+
+        def run(stage_fn, where):
+            if where is not None:
+                stage_fn(*where)
+
+        loaded = {}
+
+        def load(name, dram, n):
+            if 0 <= n < B // LOAD:
+                loaded[name, n] = load_rows(dram, n, name + "_sb")
+
+        load("liq", liq, 0)
+        wo = quantise_weight(wo_sb, "wo", u_ps, "u_acc")
+        win_sb = load_weight(W_in)
+        load("x", x, 0)
+        win_q = whole(quantise_weight(win_sb, "win", u_ps, "u_acc"))
+        load("liq", liq, 1)
+        load("h", h, 0)
+
+        for k in range(GROUPS * HALF + B0):
+            if k % TILES == 0 and k > 0:
+                load("liq", liq, k // TILES + 1)
+                load("x", x, k // TILES)
+                load("h", h, k // TILES - 1 if k > TILES else -1)
+            a = item(k, 0)
+            b = item(k, X0)
+            words = None
+            if a and a[1] == 0:
+                words = (a[0], "liq")
+            if b and b[1] == 1:
+                words = (b[0], "x")
+            run(back_turn, item(k, B0))
+            run(v_mx, item(k, V0))
+            run(att_mx, item(k, ATT0))
+            run(xin_mx, item(k, S0))
+            run(u_turn, item(k, U0))
+            run(words_stage, words)
+            run(s_turn, item(k, T0))
+            run(stats, item(k, U0))
+            run(words_copy, words)
+            run(squares, item(k, U0))
+            run(tanh_stage, item(k, T0))
+            run(out_stage, item(k, B0))
+            run(v_out, item(k, V0))
+            run(uT_out, item(k, ATT0))
+            q = item(k, V0)
+            if q and q[1] == HALF - 1:
+                quantise_stage(q[0], "v")
+            if a and a[1] == 1:
+                quantise_stage(a[0], "liq")
+            b = item(k, X0 + 2)
+            if b and b[1] == 0:
+                quantise_stage(b[0], "x")
+            run(s_out, item(k, S0))
+            run(w_out, item(k, U0))
+            run(keep_stage, item(k, B0 - 3))
+            r = item(k, U0)
+            if r and r[1] == HALF - 1:
+                rstd_stage(r[0])

@@ -51,6 +51,8 @@ def tile_advancedliquidneuralnetwork_pb_t_kernel(
 
         ident = consts.tile([P, P], F32)
         make_identity(nc, ident[:])
+        warm_bf16 = consts.tile([P, H], BF16)
+        nc.vector.memset(warm_bf16[:], 0.0)
         minus_half = consts.tile([P, HALF], F32)
         nc.vector.memset(minus_half[:], -0.5)
 
@@ -271,6 +273,10 @@ def tile_advancedliquidneuralnetwork_pb_t_kernel(
         def s_turn(g, i):
             s = st[g]
             s["sT"] = one_ps.tile([P, 2, HALF, P], F32, name="sT", tag="sT")
+            nc.tensor.matmul(
+                out=s["sT"][:].rearrange("p j t n -> p (j t n)"), lhsT=warm_bf16[:, 0:P], rhs=warm_bf16[:],
+                start=True, stop=True,
+            )
             for jj in range(2):
                 j = 2 * i + jj
                 for t in range(HALF):

@@ -35,11 +35,11 @@ def tile_advancedliquidneuralnetwork_pb_t_kernel(
 
     with ExitStack() as ctx:
         consts = ctx.enter_context(tc.tile_pool(name="consts", bufs=1))
-        rows = ctx.enter_context(tc.tile_pool(name="rows", bufs=3))
+        rows = ctx.enter_context(tc.tile_pool(name="rows", bufs=4))
         stage = ctx.enter_context(tc.tile_pool(name="stage", bufs=3))
         codes = ctx.enter_context(tc.tile_pool(name="codes", bufs=3))
         work = ctx.enter_context(tc.tile_pool(name="work", bufs=2))
-        ring = ctx.enter_context(tc.tile_pool(name="ring", bufs=5))
+        ring = ctx.enter_context(tc.tile_pool(name="ring", bufs=4))
         small = ctx.enter_context(tc.tile_pool(name="small", bufs=6))
         one_ps = ctx.enter_context(tc.psum_pool(name="one_ps", bufs=1))
         u_ps = ctx.enter_context(tc.psum_pool(name="u_ps", bufs=2))
@@ -51,10 +51,13 @@ def tile_advancedliquidneuralnetwork_pb_t_kernel(
 
         ident = consts.tile([P, P], F32)
         make_identity(nc, ident[:])
-        warm_bf16 = consts.tile([P, H], BF16)
-        nc.vector.memset(warm_bf16[:], 0.0)
+        ident_bf16 = consts.tile([P, P], BF16)
+        make_identity(nc, ident_bf16[:])
         minus_half = consts.tile([P, HALF], F32)
         nc.vector.memset(minus_half[:], -0.5)
+
+        def bf16_view(grouped):
+            return grouped[:].rearrange("p c u -> p (c u)").bitcast(BF16)
 
         def turn_words(src, pair, words):
             for i in range(2):
@@ -62,14 +65,14 @@ def tile_advancedliquidneuralnetwork_pb_t_kernel(
                 for u in range(2):
                     nc.tensor.transpose(out=words[:, i, u, :], in_=view[:, u, :], identity=ident[:])
 
-        def words_out(grouped, pair, words):
-            nc.scalar.copy(
+        def words_out(copy, grouped, pair, words):
+            copy(
                 out=grouped[:, 2 * pair * P : 2 * (pair + 1) * P, :].rearrange("p (i c) u -> p i c u", i=2),
                 in_=words[:].rearrange("p i u c -> p i c u"),
             )
 
-        def quantise(grouped_bf16, words, scales):
-            nc.vector.quantize_mx(out=words.bitcast(FP8X4), scales=scales, in_=grouped_bf16)
+        def quantise(grouped_bf16, q):
+            nc.vector.quantize_mx(out=q[0].bitcast(FP8X4), scales=q[1], in_=grouped_bf16)
 
         def mx_pass(acc, stationary, moving):
             nc.tensor.matmul_mx(
@@ -82,99 +85,117 @@ def tile_advancedliquidneuralnetwork_pb_t_kernel(
                 stop=True,
             )
 
-        def quantise_weight(w_sb, name, pool, tag):
-            grouped = stage.tile([P, H, 2], F32, align_bytes=64, name="w_grouped")
-            for pair in range(2):
-                words = pool.tile([P, 2, 2, P], F32, name="words_" + tag, tag=tag)
-                turn_words(w_sb, pair, words)
-                words_out(grouped, pair, words)
-            w_words = consts.tile([P, H], U32, align_bytes=64, name=name + "_words")
-            w_scales = consts.tile([P, H], U8, align_bytes=64, name=name + "_scales")
-            quantise(grouped[:].rearrange("p c u -> p (c u)").bitcast(BF16), w_words[:], w_scales[:])
-            return w_words, w_scales
+        def chunk(q, i):
+            return q[0][:, i * P : (i + 1) * P], q[1][:, i * P : (i + 1) * P]
 
-        def chunk(operand, i):
-            return operand[0][:, i * P : (i + 1) * P], operand[1][:, i * P : (i + 1) * P]
-
-        def load_weight(w):
-            w_sb = stage.tile([P, TILES, H], BF16, name="w_sb")
-            nc.sync.dma_start(out=w_sb[:], in_=w.rearrange("(p j) k -> p j k", j=TILES))
+        def load_weight(view, name):
+            w_sb = consts.tile([P, TILES, H], BF16, name=name + "_sb")
+            for i in range(2):
+                nc.sync.dma_start(out=w_sb[:, 2 * i : 2 * i + 2, :], in_=view[:, 2 * i : 2 * i + 2, :])
             return w_sb
 
-        def load_rows(dram, g, name):
-            sb = rows.tile([P, TILES, H], BF16, name=name)
-            nc.sync.dma_start(out=sb[:], in_=load_rows_view(dram, g))
-            return sb
+        def load(name, dram, n):
+            if 0 <= n < B // LOAD:
+                sb = rows.tile([P, TILES, H], BF16, name=name + "_sb")
+                nc.sync.dma_start(out=sb[:], in_=load_rows_view(dram, n))
+                loaded[name, n] = sb
 
-        wv_sb = load_weight(W_v)
-        vec_bf16 = consts.tile([P, 6, 16], BF16)
-        for n, vec in enumerate((b_v, b_o, b_in, beta_att, tau, g_att)):
-            nc.scalar.dma_start(out=vec_bf16[:, n, 0:TILES], in_=vec.rearrange("(p j) -> p j", j=TILES))
-        wv = quantise_weight(wv_sb, "wv", one_ps, "words")
-        wo_sb = load_weight(W_o)
-        vec_cols = consts.tile([P, 6, TILES], F32)
-        nc.vector.tensor_copy(out=vec_cols[:], in_=vec_bf16[:, :, 0:TILES])
-        bv = vec_cols[:, 0, :]
-        bo = vec_cols[:, 1, :]
+        loaded = {}
+        weights = {}
+        weights["v", "sb"] = load_weight(W_v.rearrange("(p j) k -> p j k", j=TILES), "wv")
+        load("liq", liq, 0)
+        weights["o", "sb"] = load_weight(W_o.rearrange("(a p) k -> p a k", p=P), "wo")
+        load("liq", liq, 1)
+        weights["in", "sb"] = load_weight(W_in.rearrange("(a p) k -> p a k", p=P), "win")
+        load("x", x, 0)
+        load("h", h, 0)
+
+        bv_bf16 = consts.tile([P, TILES], BF16)
+        nc.scalar.dma_start(out=bv_bf16[:], in_=b_v.rearrange("(p j) -> p j", j=TILES))
+        vec_rows = consts.tile([P, P], BF16)
+        nc.vector.memset(vec_rows[:], 0.0)
+        for n, vec in enumerate((b_o, b_in, beta_att, tau, g_att)):
+            nc.scalar.dma_start(
+                out=vec_rows[n * TILES : (n + 1) * TILES, :], in_=vec.rearrange("(j p) -> j p", p=P)
+            )
+
+        def weight_words(name, pair, tag, copy):
+            w = weights
+            if pair == 0:
+                w[name, "grouped"] = stage.tile([P, H, 2], F32, align_bytes=64, name="w_grouped")
+            pool = u_ps if tag == "u" else one_ps
+            words = pool.tile([P, 2, 2, P], F32, name="w_words", tag=tag)
+            turn_words(w[name, "sb"], pair, words)
+            words_out(copy, w[name, "grouped"], pair, words)
+
+        def weight_quantise(name):
+            q = (
+                consts.tile([P, H], U32, align_bytes=64, name="w" + name + "_words"),
+                consts.tile([P, H], U8, align_bytes=64, name="w" + name + "_scales"),
+            )
+            weights[name] = (q[0][:], q[1][:])
+            quantise(bf16_view(weights[name, "grouped"]), weights[name])
+
+        weight_words("v", 0, "att", nc.scalar.copy)
+        weight_words("v", 1, "xin", nc.vector.tensor_copy)
+        weight_quantise("v")
+        bv = consts.tile([P, TILES], F32)
+        nc.vector.tensor_copy(out=bv[:], in_=bv_bf16[:])
+
+        cols = consts.tile([P, 5, TILES], F32)
         tanh_bias = consts.tile([P, TILES], F32)
-        nc.vector.tensor_add(out=tanh_bias[:], in0=vec_cols[:, 2, :], in1=vec_cols[:, 3, :])
         gate = consts.tile([P, TILES], F32)
-        nc.vector.tensor_scalar_add(out=gate[:], in0=vec_cols[:, 4, :], scalar1=TAU_EPS)
-        nc.vector.reciprocal(out=gate[:], in_=gate[:])
         keep = consts.tile([P, TILES], F32)
-        nc.vector.tensor_scalar(out=keep[:], in0=gate[:], scalar1=-1.0, scalar2=1.0, op0=ALU.mult, op1=ALU.add)
-        gain = vec_cols[:, 5, :]
         g_all = consts.tile([P, H], F32)
-        g_ps = one_ps.tile([P, TILES, P], F32, name="g_ps", tag="back")
-        for j in range(TILES):
-            nc.tensor.transpose(
-                out=g_ps[:, j, :], in_=gain[:, j : j + 1].to_broadcast([P, P]), identity=ident[:]
-            )
-        nc.vector.tensor_copy(out=g_all[:], in_=g_ps[:].rearrange("p j m -> p (j m)"))
         keep_all = consts.tile([P, H], F32)
-        k_ps = one_ps.tile([P, TILES, P], F32, name="k_ps", tag="sT")
-        for j in range(TILES):
-            nc.tensor.transpose(
-                out=k_ps[:, j, :], in_=keep[:, j : j + 1].to_broadcast([P, P]), identity=ident[:]
+
+        def vectors():
+            vec_ps = one_ps.tile([P, P], BF16, name="vec_ps", tag="back")
+            nc.tensor.transpose(out=vec_ps[:], in_=vec_rows[:], identity=ident_bf16[:])
+            nc.vector.tensor_copy(
+                out=cols[:].rearrange("p n j -> p (n j)"), in_=vec_ps[:, 0 : 5 * TILES]
             )
-        nc.vector.tensor_copy(
-            out=keep_all[:].rearrange("p (m j) -> p m j", j=TILES), in_=k_ps[:].rearrange("p j m -> p m j")
-        )
+            nc.vector.tensor_add(out=tanh_bias[:], in0=cols[:, 1, :], in1=cols[:, 2, :])
+            nc.vector.tensor_scalar_add(out=gate[:], in0=cols[:, 3, :], scalar1=TAU_EPS)
+            nc.vector.reciprocal(out=gate[:], in_=gate[:])
+            nc.vector.tensor_scalar(
+                out=keep[:], in0=gate[:], scalar1=-1.0, scalar2=1.0, op0=ALU.mult, op1=ALU.add
+            )
+
+        def spread(column, dst, tag):
+            ps = one_ps.tile([P, TILES, P], F32, name="spread", tag=tag)
+            for j in range(TILES):
+                nc.tensor.transpose(
+                    out=ps[:, j, :], in_=column[:, j : j + 1].to_broadcast([P, P]), identity=ident[:]
+                )
+            nc.scalar.copy(out=dst[:], in_=ps[:].rearrange("p j m -> p (j m)"))
 
         st = [{} for g in range(GROUPS)]
 
-        def codes_tile(name):
-            return (
-                codes.tile([P, GROUP], U32, align_bytes=64, name=name + "_words"),
-                codes.tile([P, GROUP], U8, align_bytes=64, name=name + "_scales"),
-            )
-
-        def whole(q):
-            return q[0][:], q[1][:]
-
-        def bf16_view(grouped):
-            return grouped[:].rearrange("p c u -> p (c u)").bitcast(BF16)
-
-        def words_stage(g, name):
+        def words_turn(g, name):
             s = st[g]
             s[name + "T"] = stage.tile([P, GROUP, 2], F32, align_bytes=64, name=name + "T")
             s["words"] = one_ps.tile([P, 2, 2, P], F32, name="words", tag="words")
             turn_words(loaded[name, g // 2], g % 2, s["words"])
 
         def words_copy(g, name):
-            words_out(st[g][name + "T"], 0, st[g]["words"])
+            words_out(nc.scalar.copy, st[g][name + "T"], 0, st[g]["words"])
 
         def quantise_stage(g, name):
             s = st[g]
-            s[name + "_q"] = codes_tile(name)
+            q = (
+                codes.tile([P, GROUP], U32, align_bytes=64, name=name + "_words"),
+                codes.tile([P, GROUP], U8, align_bytes=64, name=name + "_scales"),
+            )
+            s[name + "_q"] = (q[0][:], q[1][:])
             src = s["v_bf16"][:].rearrange("p n j -> p (n j)") if name == "v" else bf16_view(s[name + "T"])
-            quantise(src, *whole(s[name + "_q"]))
+            quantise(src, s[name + "_q"])
 
         def v_mx(g, t):
             s = st[g]
             s["v_acc"] = one_ps.tile([P, TILES, P], F32, name="v_acc", tag="v_acc")
             for j in range(TILES):
-                mx_pass(s["v_acc"][:, j, :], chunk(wv, j), chunk(s["liq_q"], t))
+                mx_pass(s["v_acc"][:, j, :], chunk(weights["v"], j), chunk(s["liq_q"], t))
 
         def v_out(g, t):
             s = st[g]
@@ -183,7 +204,7 @@ def tile_advancedliquidneuralnetwork_pb_t_kernel(
             nc.vector.tensor_tensor(
                 out=s["v_bf16"][:, t * P : (t + 1) * P, :],
                 in0=s["v_acc"][:].rearrange("p j n -> p n j"),
-                in1=bv.unsqueeze(1).to_broadcast([P, P, TILES]),
+                in1=bv[:].unsqueeze(1).to_broadcast([P, P, TILES]),
                 op=ALU.add,
             )
 
@@ -191,77 +212,93 @@ def tile_advancedliquidneuralnetwork_pb_t_kernel(
             s = st[g]
             s["att"] = one_ps.tile([P, 2, GROUP], F32, name="att", tag="att")
             for jj in range(2):
-                mx_pass(s["att"][:, jj, :], chunk(wo, 2 * i + jj), whole(s["v_q"]))
+                mx_pass(s["att"][:, jj, :], chunk(weights["o"], 2 * i + jj), s["v_q"])
 
-        def uT_out(g, i):
+        def att_out(g, i):
             s = st[g]
             if i == 0:
-                s["uT"] = work.tile([P, TILES, GROUP], F32, name="uT")
+                s["attT"] = work.tile([P, TILES, GROUP], F32, name="attT")
             for jj in range(2):
                 j = 2 * i + jj
-                nc.vector.scalar_tensor_tensor(
-                    out=s["uT"][:, j, :],
-                    in0=s["att"][:, jj, :],
-                    scalar=bo[:, j : j + 1],
-                    in1=bf16_view(s["liqT"]).rearrange("p (n j) -> p j n", j=TILES)[:, j, :],
-                    op0=ALU.add,
-                    op1=ALU.add,
+                nc.scalar.activation(
+                    out=s["attT"][:, j, :], in_=s["att"][:, jj, :], func=ACT.Identity, bias=cols[:, 0, j : j + 1]
                 )
 
-        def u_turn(g, t):
+        def u_sum(g, t):
             s = st[g]
-            u_acc = u_ps.tile([P, TILES, P], F32, name="u_acc", tag="u_acc")
+            u = u_ps.tile([P, H], F32, name="u", tag="u")
+            s["u", t] = u
+            nc.tensor.matmul(
+                out=u[:], lhsT=ident_bf16[:], rhs=loaded["liq", g // 2][:, 2 * (g % 2) + t, :], start=True, stop=False
+            )
             for j in range(TILES):
-                nc.tensor.transpose(
-                    out=u_acc[:, j, :], in_=s["uT"][:, j, t * P : (t + 1) * P], identity=ident[:]
+                nc.tensor.matmul(
+                    out=u[:, j * P : (j + 1) * P], lhsT=s["attT"][:, j, t * P : (t + 1) * P], rhs=ident[:],
+                    is_transpose=True, start=False, stop=j == TILES - 1,
                 )
-            s["u", t] = u_acc[:].rearrange("p j m -> p (j m)")
 
-        def stats(g, t):
+        def sum_stage(g, t):
             s = st[g]
+            if t == 0:
+                s["var"] = small.tile([P, HALF], F32, name="var")
+            if t in BN:
+                return
             s["neg_mean", t] = small.tile([P, 1], F32, name="neg_mean")
             unused = work.tile([P, H], BF16, name="unused")
             nc.scalar.activation(
-                out=unused[:], in_=s["u", t], func=ACT.Copy, scale=-1.0 / H, accum_out=s["neg_mean", t][:]
+                out=unused[:], in_=s["u", t][:], func=ACT.Copy, scale=-1.0 / H, accum_out=s["neg_mean", t][:]
             )
 
-        def squares(g, t):
+        def squares_stage(g, t):
             s = st[g]
-            if t == 0:
-                s["sum_sq"] = small.tile([P, HALF], F32, name="sum_sq")
+            if t in BN:
+                return
+            s["sum_sq", t] = small.tile([P, 1], F32, name="sum_sq")
             unused = work.tile([P, H], BF16, name="unused")
             nc.scalar.activation(
-                out=unused[:],
-                in_=s["u", t],
-                func=ACT.Square,
-                bias=s["neg_mean", t][:],
-                accum_out=s["sum_sq"][:, t : t + 1],
+                out=unused[:], in_=s["u", t][:], func=ACT.Square, bias=s["neg_mean", t][:],
+                accum_out=s["sum_sq", t][:],
             )
+
+        def bn_stage(g, t):
+            s = st[g]
+            if t in BN:
+                s["stats"] = small.tile([P, 6], F32, name="stats")
+                nc.vector.bn_stats(out=s["stats"][:], in_=s["u", t][:])
+
+        def bn_end(g, t):
+            s = st[g]
+            if t in BN:
+                s["mean_var", t] = small.tile([P, 2], F32, name="mean_var")
+                nc.vector.bn_aggr(out=s["mean_var", t][:], in_=s["stats"][:])
 
         def rstd_stage(g):
             s = st[g]
             r = small.tile([P, HALF], F32, name="rstd")
             s["rstd"] = r
-            nc.gpsimd.tensor_scalar(
-                out=r[:], in0=s["sum_sq"][:], scalar1=1.0 / H, scalar2=LN_EPS,
-                op0=ALU.mult, op1=ALU.add,
-            )
+            for t in range(HALF):
+                src = s["mean_var", t][:, 1:2] if t in BN else s["sum_sq", t][:]
+                nc.gpsimd.tensor_scalar(
+                    out=r[:, t : t + 1], in0=src, scalar1=1.0 if t in BN else 1.0 / H, scalar2=LN_EPS,
+                    op0=ALU.mult, op1=ALU.add,
+                )
             nc.gpsimd.tensor_tensor(out=r[:], in0=r[:], in1=minus_half[:], op=ALU.pow)
 
-        def w_out(g, t):
+        def w_stage(g, t):
             s = st[g]
             s["w", t] = ring.tile([P, H], F32, name="w")
             nc.vector.scalar_tensor_tensor(
-                out=s["w", t][:], in0=s["u", t], scalar=s["neg_mean", t][:], in1=g_all[:],
-                op0=ALU.add, op1=ALU.mult,
+                out=s["w", t][:], in0=s["u", t][:],
+                scalar=s["mean_var", t][:, 0:1] if t in BN else s["neg_mean", t][:],
+                in1=g_all[:], op0=ALU.subtract if t in BN else ALU.add, op1=ALU.mult,
             )
 
         def xin_mx(g, t):
             s = st[g]
             s["xin"] = one_ps.tile([P, H], F32, name="xin", tag="xin")
-            mx_pass(s["xin"][:], chunk(s["x_q"], t), win_q)
+            mx_pass(s["xin"][:], chunk(s["x_q"], t), weights["in"])
 
-        def s_out(g, t):
+        def s_stage(g, t):
             s = st[g]
             if t == 0:
                 s["s"] = work.tile([P, HALF, H], F32, name="s")
@@ -273,10 +310,6 @@ def tile_advancedliquidneuralnetwork_pb_t_kernel(
         def s_turn(g, i):
             s = st[g]
             s["sT"] = one_ps.tile([P, 2, HALF, P], F32, name="sT", tag="sT")
-            nc.tensor.matmul(
-                out=s["sT"][:].rearrange("p j t n -> p (j t n)"), lhsT=warm_bf16[:, 0:P], rhs=warm_bf16[:],
-                start=True, stop=True,
-            )
             for jj in range(2):
                 j = 2 * i + jj
                 for t in range(HALF):
@@ -286,54 +319,48 @@ def tile_advancedliquidneuralnetwork_pb_t_kernel(
 
         def tanh_stage(g, i):
             s = st[g]
+            s["tanhT"] = work.tile([P, 2, GROUP], F32, name="tanhT")
+            for jj in range(2):
+                j = 2 * i + jj
+                nc.scalar.activation(
+                    out=s["tanhT"][:, jj, :], in_=s["sT"][:, jj, :, :].rearrange("p t n -> p (t n)"),
+                    func=ACT.Tanh, bias=tanh_bias[:, j : j + 1],
+                )
+
+        def gate_stage(g, i):
+            s = st[g]
             if i == 0:
                 s["gatedT"] = work.tile([P, TILES, GROUP], F32, name="gatedT")
-            tanhT = work.tile([P, 2, GROUP], F32, name="tanhT")
             for jj in range(2):
                 j = 2 * i + jj
                 nc.scalar.activation(
-                    out=tanhT[:, jj, :], in_=s["sT"][:, jj, :, :].rearrange("p t n -> p (t n)"), func=ACT.Tanh,
-                    bias=tanh_bias[:, j : j + 1],
-                )
-            for jj in range(2):
-                j = 2 * i + jj
-                nc.scalar.activation(
-                    out=s["gatedT"][:, j, :], in_=tanhT[:, jj, :], func=ACT.Copy, scale=gate[:, j : j + 1]
+                    out=s["gatedT"][:, j, :], in_=s["tanhT"][:, jj, :], func=ACT.Copy, scale=gate[:, j : j + 1]
                 )
 
         def keep_stage(g, t):
             s = st[g]
-            s["h_kept", t] = ring.tile([P, H], F32, name="h_kept")
+            s["h_kept", t] = ring.tile([P, H], F32, name="h_kept", bufs=3)
             nc.gpsimd.tensor_tensor(
                 out=s["h_kept", t][:], in0=loaded["h", g // 2][:, 2 * (g % 2) + t, :], in1=keep_all[:], op=ALU.mult
             )
 
         def back_turn(g, t):
             s = st[g]
-            s["back"] = one_ps.tile([P, TILES, P], F32, name="back", tag="back")
+            s["back"] = one_ps.tile([P, H], F32, name="back", tag="back")
             for j in range(TILES):
                 nc.tensor.transpose(
-                    out=s["back"][:, j, :], in_=s["gatedT"][:, j, t * P : (t + 1) * P], identity=ident[:]
+                    out=s["back"][:, j * P : (j + 1) * P], in_=s["gatedT"][:, j, t * P : (t + 1) * P],
+                    identity=ident[:],
                 )
 
         def out_stage(g, t):
             s = st[g]
             if t == 0:
                 s["out"] = work.tile([P, HALF, H], F32, name="out_sb")
-            nc.vector.tensor_tensor(
-                out=s["out"][:, t, :].rearrange("p (m j) -> p m j", j=TILES),
-                in0=s["back"][:].rearrange("p j m -> p m j"),
-                in1=s["h_kept", t][:].rearrange("p (m j) -> p m j", j=TILES),
-                op=ALU.add,
-            )
+            nc.vector.tensor_tensor(out=s["out"][:, t, :], in0=s["back"][:], in1=s["h_kept", t][:], op=ALU.add)
             if t == HALF - 1:
                 first = 2 * (g % 2)
-                nc.sync.dma_start(
-                    out=load_rows_view(out, g // 2)[:, first : first + HALF, :], in_=s["out"][:]
-                )
-
-        X0 = 4
-        V0, ATT0, U0, S0, T0, B0 = 2, 4, 6, 8, 10, 13
+                nc.sync.dma_start(out=load_rows_view(out, g // 2)[:, first : first + HALF, :], in_=s["out"][:])
 
         def item(k, first):
             n = k - first
@@ -343,25 +370,10 @@ def tile_advancedliquidneuralnetwork_pb_t_kernel(
             if where is not None:
                 stage_fn(*where)
 
-        loaded = {}
-
-        def load(name, dram, n):
-            if 0 <= n < B // LOAD:
-                loaded[name, n] = load_rows(dram, n, name + "_sb")
-
-        load("liq", liq, 0)
-        wo = quantise_weight(wo_sb, "wo", u_ps, "u_acc")
-        win_sb = load_weight(W_in)
-        load("x", x, 0)
-        win_q = whole(quantise_weight(win_sb, "win", u_ps, "u_acc"))
-        load("liq", liq, 1)
-        load("h", h, 0)
-
+        BN = (0,)
+        X0 = 4
+        V0, ATT0, U0, W0, S0, T0, B0 = 2, 4, 6, 7, 9, 11, 13
         for k in range(GROUPS * HALF + B0):
-            if k % TILES == 0 and k > 0:
-                load("liq", liq, k // TILES + 1)
-                load("x", x, k // TILES)
-                load("h", h, k // TILES - 1 if k > TILES else -1)
             a = item(k, 0)
             b = item(k, X0)
             words = None
@@ -369,21 +381,43 @@ def tile_advancedliquidneuralnetwork_pb_t_kernel(
                 words = (a[0], "liq")
             if b and b[1] == 1:
                 words = (b[0], "x")
-            run(back_turn, item(k, B0))
+            if k % TILES == 0 and k > 0:
+                load("liq", liq, k // TILES + 1)
+                load("x", x, k // TILES)
+                load("h", h, k // TILES - 1 if k > TILES else -1)
+            run(xin_mx, item(k, S0))
             run(v_mx, item(k, V0))
             run(att_mx, item(k, ATT0))
-            run(xin_mx, item(k, S0))
-            run(u_turn, item(k, U0))
-            run(words_stage, words)
+            if k > 0:
+                run(words_turn, words)
+            run(u_sum, item(k, U0))
+            if k == 0:
+                words_turn(*words)
+                weight_words("o", 0, "u", nc.vector.tensor_copy)
+                weight_words("o", 1, "u", nc.scalar.copy)
+                vectors()
+            elif k == 3:
+                weight_words("in", 0, "xin", nc.scalar.copy)
+            elif k == 4:
+                weight_words("in", 1, "sT", nc.scalar.copy)
+            elif k == 1:
+                spread(cols[:, 4, :], g_all, "sT")
+            elif k == 2:
+                spread(keep, keep_all, "back")
+            run(back_turn, item(k, B0))
             run(s_turn, item(k, T0))
-            run(stats, item(k, U0))
+            run(sum_stage, item(k, W0))
+            run(att_out, item(k, ATT0))
+            run(squares_stage, item(k, W0))
             run(words_copy, words)
-            run(squares, item(k, U0))
             run(tanh_stage, item(k, T0))
-            run(out_stage, item(k, B0))
+            run(gate_stage, item(k, T0))
+            run(bn_stage, item(k, W0))
+            run(s_stage, item(k, S0))
             run(v_out, item(k, V0))
-            run(uT_out, item(k, ATT0))
-            q = item(k, V0)
+            run(bn_end, item(k, W0))
+            run(w_stage, item(k, W0))
+            q = item(k, V0 + 0)
             if q and q[1] == HALF - 1:
                 quantise_stage(q[0], "v")
             if a and a[1] == 1:
@@ -391,9 +425,12 @@ def tile_advancedliquidneuralnetwork_pb_t_kernel(
             b = item(k, X0 + 2)
             if b and b[1] == 0:
                 quantise_stage(b[0], "x")
-            run(s_out, item(k, S0))
-            run(w_out, item(k, U0))
-            run(keep_stage, item(k, B0 - 3))
-            r = item(k, U0)
+            if k == 1:
+                weight_quantise("o")
+            elif k == 5:
+                weight_quantise("in")
+            run(out_stage, item(k, B0))
+            r = item(k, W0)
             if r and r[1] == HALF - 1:
                 rstd_stage(r[0])
+            run(keep_stage, item(k, B0 - 3))

@@ -20,6 +20,8 @@ HALF = 2
 GROUP = HALF * P
 GROUPS = B // GROUP
 LN_EPS = 1e-5
+DUMMY = 64
+KB = 6
 TAU_EPS = 1e-6
 
 FLOPS = 3 * 2 * B * H * H
@@ -36,13 +38,13 @@ def tile_advancedliquidneuralnetwork_pb_t_kernel(
     with ExitStack() as ctx:
         consts = ctx.enter_context(tc.tile_pool(name="consts", bufs=1))
         rows = ctx.enter_context(tc.tile_pool(name="rows", bufs=4))
-        stage = ctx.enter_context(tc.tile_pool(name="stage", bufs=3))
-        codes = ctx.enter_context(tc.tile_pool(name="codes", bufs=3))
+        stage = ctx.enter_context(tc.tile_pool(name="stage", bufs=4))
+        codes = ctx.enter_context(tc.tile_pool(name="codes", bufs=4))
         work = ctx.enter_context(tc.tile_pool(name="work", bufs=2))
-        ring = ctx.enter_context(tc.tile_pool(name="ring", bufs=4))
+        kept = ctx.enter_context(tc.tile_pool(name="kept", bufs=1))
         small = ctx.enter_context(tc.tile_pool(name="small", bufs=6))
-        one_ps = ctx.enter_context(tc.psum_pool(name="one_ps", bufs=1))
-        u_ps = ctx.enter_context(tc.psum_pool(name="u_ps", bufs=2))
+        psum = ctx.enter_context(tc.psum_pool(name="psum", bufs=2))
+        BUFS = {"words": 1, "first": 2, "second": 2, "turned": 3}
         ctx.enter_context(tc.manual_schedule())
 
         warm = consts.tile([P, 1], F32)
@@ -96,7 +98,7 @@ def tile_advancedliquidneuralnetwork_pb_t_kernel(
 
         def load(name, dram, n):
             if 0 <= n < B // LOAD:
-                sb = rows.tile([P, TILES, H], BF16, name=name + "_sb")
+                sb = rows.tile([P, TILES, H], BF16, name=name + "_sb", bufs=5 if name == "liq" else 3)
                 nc.sync.dma_start(out=sb[:], in_=load_rows_view(dram, n))
                 loaded[name, n] = sb
 
@@ -107,8 +109,6 @@ def tile_advancedliquidneuralnetwork_pb_t_kernel(
         weights["o", "sb"] = load_weight(W_o.rearrange("(a p) k -> p a k", p=P), "wo")
         load("liq", liq, 1)
         weights["in", "sb"] = load_weight(W_in.rearrange("(a p) k -> p a k", p=P), "win")
-        load("x", x, 0)
-        load("h", h, 0)
 
         bv_bf16 = consts.tile([P, TILES], BF16)
         nc.scalar.dma_start(out=bv_bf16[:], in_=b_v.rearrange("(p j) -> p j", j=TILES))
@@ -122,9 +122,8 @@ def tile_advancedliquidneuralnetwork_pb_t_kernel(
         def weight_words(name, pair, tag, copy):
             w = weights
             if pair == 0:
-                w[name, "grouped"] = stage.tile([P, H, 2], F32, align_bytes=64, name="w_grouped")
-            pool = u_ps if tag == "u" else one_ps
-            words = pool.tile([P, 2, 2, P], F32, name="w_words", tag=tag)
+                w[name, "grouped"] = stage.tile([P, H, 2], F32, align_bytes=64, name="w_grouped", bufs=2)
+            words = psum.tile([P, 2, 2, P], F32, name="w_words", tag=tag, bufs=BUFS[tag])
             turn_words(w[name, "sb"], pair, words)
             words_out(copy, w[name, "grouped"], pair, words)
 
@@ -136,8 +135,8 @@ def tile_advancedliquidneuralnetwork_pb_t_kernel(
             weights[name] = (q[0][:], q[1][:])
             quantise(bf16_view(weights[name, "grouped"]), weights[name])
 
-        weight_words("v", 0, "att", nc.scalar.copy)
-        weight_words("v", 1, "xin", nc.vector.tensor_copy)
+        weight_words("v", 0, "turned", nc.scalar.copy)
+        weight_words("v", 1, "turned", nc.vector.tensor_copy)
         weight_quantise("v")
         bv = consts.tile([P, TILES], F32)
         nc.vector.tensor_copy(out=bv[:], in_=bv_bf16[:])
@@ -150,7 +149,7 @@ def tile_advancedliquidneuralnetwork_pb_t_kernel(
         keep_all = consts.tile([P, H], F32)
 
         def vectors():
-            vec_ps = one_ps.tile([P, P], BF16, name="vec_ps", tag="back")
+            vec_ps = psum.tile([P, P], BF16, name="vec_ps", tag="turned", bufs=BUFS["turned"])
             nc.tensor.transpose(out=vec_ps[:], in_=vec_rows[:], identity=ident_bf16[:])
             nc.vector.tensor_copy(
                 out=cols[:].rearrange("p n j -> p (n j)"), in_=vec_ps[:, 0 : 5 * TILES]
@@ -163,7 +162,7 @@ def tile_advancedliquidneuralnetwork_pb_t_kernel(
             )
 
         def spread(column, dst, tag):
-            ps = one_ps.tile([P, TILES, P], F32, name="spread", tag=tag)
+            ps = psum.tile([P, TILES, P], F32, name="spread", tag=tag)
             for j in range(TILES):
                 nc.tensor.transpose(
                     out=ps[:, j, :], in_=column[:, j : j + 1].to_broadcast([P, P]), identity=ident[:]
@@ -175,7 +174,7 @@ def tile_advancedliquidneuralnetwork_pb_t_kernel(
         def words_turn(g, name):
             s = st[g]
             s[name + "T"] = stage.tile([P, GROUP, 2], F32, align_bytes=64, name=name + "T")
-            s["words"] = one_ps.tile([P, 2, 2, P], F32, name="words", tag="words")
+            s["words"] = psum.tile([P, 2, 2, P], F32, name="words", tag="words", bufs=BUFS["words"])
             turn_words(loaded[name, g // 2], g % 2, s["words"])
 
         def words_copy(g, name):
@@ -193,7 +192,7 @@ def tile_advancedliquidneuralnetwork_pb_t_kernel(
 
         def v_mx(g, t):
             s = st[g]
-            s["v_acc"] = one_ps.tile([P, TILES, P], F32, name="v_acc", tag="v_acc")
+            s["v_acc"] = psum.tile([P, TILES, P], F32, name="v_acc", tag="first", bufs=BUFS["first"])
             for j in range(TILES):
                 mx_pass(s["v_acc"][:, j, :], chunk(weights["v"], j), chunk(s["liq_q"], t))
 
@@ -210,7 +209,7 @@ def tile_advancedliquidneuralnetwork_pb_t_kernel(
 
         def att_mx(g, i):
             s = st[g]
-            s["att"] = one_ps.tile([P, 2, GROUP], F32, name="att", tag="att")
+            s["att"] = psum.tile([P, 2, GROUP], F32, name="att", tag="second", bufs=BUFS["second"])
             for jj in range(2):
                 mx_pass(s["att"][:, jj, :], chunk(weights["o"], 2 * i + jj), s["v_q"])
 
@@ -226,7 +225,7 @@ def tile_advancedliquidneuralnetwork_pb_t_kernel(
 
         def u_sum(g, t):
             s = st[g]
-            u = u_ps.tile([P, H], F32, name="u", tag="u")
+            u = psum.tile([P, H], F32, name="u", tag="turned", bufs=BUFS["turned"])
             s["u", t] = u
             nc.tensor.matmul(
                 out=u[:], lhsT=ident_bf16[:], rhs=loaded["liq", g // 2][:, 2 * (g % 2) + t, :], start=True, stop=False
@@ -274,7 +273,7 @@ def tile_advancedliquidneuralnetwork_pb_t_kernel(
 
         def rstd_stage(g):
             s = st[g]
-            r = small.tile([P, HALF], F32, name="rstd")
+            r = kept.tile([P, HALF], F32, name="rstd%d" % g)
             s["rstd"] = r
             for t in range(HALF):
                 src = s["mean_var", t][:, 1:2] if t in BN else s["sum_sq", t][:]
@@ -286,35 +285,35 @@ def tile_advancedliquidneuralnetwork_pb_t_kernel(
 
         def w_stage(g, t):
             s = st[g]
-            s["w", t] = ring.tile([P, H], F32, name="w")
+            if t == 0:
+                s["w"] = kept.tile([P, HALF, H], F32, name="w%d" % g)
             nc.vector.scalar_tensor_tensor(
-                out=s["w", t][:], in0=s["u", t][:],
+                out=s["w"][:, t, :], in0=s["u", t][:],
                 scalar=s["mean_var", t][:, 0:1] if t in BN else s["neg_mean", t][:],
                 in1=g_all[:], op0=ALU.subtract if t in BN else ALU.add, op1=ALU.mult,
             )
 
         def xin_mx(g, t):
             s = st[g]
-            s["xin"] = one_ps.tile([P, H], F32, name="xin", tag="xin")
+            s["xin"] = psum.tile([P, H], F32, name="xin", tag="first", bufs=BUFS["first"])
+            nc.tensor.matmul(out=s["xin"][:, 0:DUMMY], lhsT=ident[:], rhs=ident[:, 0:DUMMY], start=True, stop=True)
             mx_pass(s["xin"][:], chunk(s["x_q"], t), weights["in"])
 
         def s_stage(g, t):
             s = st[g]
-            if t == 0:
-                s["s"] = work.tile([P, HALF, H], F32, name="s")
             nc.vector.scalar_tensor_tensor(
-                out=s["s"][:, t, :], in0=s["w", t][:], scalar=s["rstd"][:, t : t + 1],
+                out=s["w"][:, t, :], in0=s["w"][:, t, :], scalar=s["rstd"][:, t : t + 1],
                 in1=s["xin"][:], op0=ALU.mult, op1=ALU.add,
             )
 
         def s_turn(g, i):
             s = st[g]
-            s["sT"] = one_ps.tile([P, 2, HALF, P], F32, name="sT", tag="sT")
+            s["sT"] = psum.tile([P, 2, HALF, P], F32, name="sT", tag="second", bufs=BUFS["second"])
             for jj in range(2):
                 j = 2 * i + jj
                 for t in range(HALF):
                     nc.tensor.transpose(
-                        out=s["sT"][:, jj, t, :], in_=s["s"][:, t, j * P : (j + 1) * P], identity=ident[:]
+                        out=s["sT"][:, jj, t, :], in_=s["w"][:, t, j * P : (j + 1) * P], identity=ident[:]
                     )
 
         def tanh_stage(g, i):
@@ -339,14 +338,14 @@ def tile_advancedliquidneuralnetwork_pb_t_kernel(
 
         def keep_stage(g, t):
             s = st[g]
-            s["h_kept", t] = ring.tile([P, H], F32, name="h_kept", bufs=3)
+            s["h_kept", t] = kept.tile([P, H], F32, name="h_kept", bufs=KB)
             nc.gpsimd.tensor_tensor(
                 out=s["h_kept", t][:], in0=loaded["h", g // 2][:, 2 * (g % 2) + t, :], in1=keep_all[:], op=ALU.mult
             )
 
         def back_turn(g, t):
             s = st[g]
-            s["back"] = one_ps.tile([P, H], F32, name="back", tag="back")
+            s["back"] = psum.tile([P, H], F32, name="back", tag="turned", bufs=BUFS["turned"])
             for j in range(TILES):
                 nc.tensor.transpose(
                     out=s["back"][:, j * P : (j + 1) * P], in_=s["gatedT"][:, j, t * P : (t + 1) * P],
@@ -371,45 +370,49 @@ def tile_advancedliquidneuralnetwork_pb_t_kernel(
                 stage_fn(*where)
 
         BN = (0,)
-        X0 = 4
-        V0, ATT0, U0, W0, S0, T0, B0 = 2, 4, 6, 7, 9, 11, 13
-        for k in range(GROUPS * HALF + B0):
+        X0 = 42
+        H0 = 46
+        V0, ATT0, U0, W0, S0, T0, B0 = 4, 8, 11, 12, 46, 48, 50
+        for k in range(B0 + GROUPS * HALF):
             a = item(k, 0)
             b = item(k, X0)
-            words = None
-            if a and a[1] == 0:
-                words = (a[0], "liq")
-            if b and b[1] == 1:
-                words = (b[0], "x")
+            words = (0, "liq")
             if k % TILES == 0 and k > 0:
                 load("liq", liq, k // TILES + 1)
-                load("x", x, k // TILES)
-                load("h", h, k // TILES - 1 if k > TILES else -1)
-            run(xin_mx, item(k, S0))
+            if (k - X0 + 6) % TILES == 0:
+                load("x", x, (k - X0 + 6) // TILES)
+            if (k - H0 + 6) % TILES == 0:
+                load("h", h, (k - H0 + 6) // TILES)
             run(v_mx, item(k, V0))
             run(att_mx, item(k, ATT0))
-            if k > 0:
-                run(words_turn, words)
-            run(u_sum, item(k, U0))
+            run(xin_mx, item(k, S0))
             if k == 0:
                 words_turn(*words)
-                weight_words("o", 0, "u", nc.vector.tensor_copy)
-                weight_words("o", 1, "u", nc.scalar.copy)
+                weight_words("o", 0, "first", nc.vector.tensor_copy)
+                weight_words("o", 1, "first", nc.scalar.copy)
                 vectors()
-            elif k == 3:
-                weight_words("in", 0, "xin", nc.scalar.copy)
-            elif k == 4:
-                weight_words("in", 1, "sT", nc.scalar.copy)
+            elif k == 5:
+                weight_words("in", 0, "second", nc.scalar.copy)
+            elif k == 6:
+                weight_words("in", 1, "second", nc.scalar.copy)
             elif k == 1:
-                spread(cols[:, 4, :], g_all, "sT")
+                spread(cols[:, 4, :], g_all, "second")
             elif k == 2:
-                spread(keep, keep_all, "back")
+                spread(keep, keep_all, "second")
+            if a and k > 0 and a[1] == 0:
+                words_turn(a[0], "liq")
+            if b and b[1] == 0:
+                words_turn(b[0], "x")
+            run(u_sum, item(k, U0))
             run(back_turn, item(k, B0))
             run(s_turn, item(k, T0))
             run(sum_stage, item(k, W0))
             run(att_out, item(k, ATT0))
             run(squares_stage, item(k, W0))
-            run(words_copy, words)
+            if a and a[1] == 0:
+                words_copy(a[0], "liq")
+            if b and b[1] == 0:
+                words_copy(b[0], "x")
             run(tanh_stage, item(k, T0))
             run(gate_stage, item(k, T0))
             run(bn_stage, item(k, W0))
@@ -417,20 +420,19 @@ def tile_advancedliquidneuralnetwork_pb_t_kernel(
             run(v_out, item(k, V0))
             run(bn_end, item(k, W0))
             run(w_stage, item(k, W0))
-            q = item(k, V0 + 0)
+            q = item(k, V0)
             if q and q[1] == HALF - 1:
                 quantise_stage(q[0], "v")
             if a and a[1] == 1:
                 quantise_stage(a[0], "liq")
-            b = item(k, X0 + 2)
-            if b and b[1] == 0:
+            if b and b[1] == 1:
                 quantise_stage(b[0], "x")
             if k == 1:
                 weight_quantise("o")
-            elif k == 5:
+            elif k == 8:
                 weight_quantise("in")
             run(out_stage, item(k, B0))
             r = item(k, W0)
             if r and r[1] == HALF - 1:
                 rstd_stage(r[0])
-            run(keep_stage, item(k, B0 - 3))
+            run(keep_stage, item(k, H0))

@@ -20,7 +20,6 @@ HALF = 2
 GROUP = HALF * P
 GROUPS = B // GROUP
 LN_EPS = 1e-5
-DUMMY = 64
 KB = 6
 TAU_EPS = 1e-6
 
@@ -296,8 +295,8 @@ def tile_advancedliquidneuralnetwork_pb_t_kernel(
         def xin_mx(g, t):
             s = st[g]
             s["xin"] = psum.tile([P, H], F32, name="xin", tag="first", bufs=BUFS["first"])
-            nc.tensor.matmul(out=s["xin"][:, 0:DUMMY], lhsT=ident[:], rhs=ident[:, 0:DUMMY], start=True, stop=True)
-            mx_pass(s["xin"][:], chunk(s["x_q"], t), weights["in"])
+            for again in range(2):
+                mx_pass(s["xin"][:], chunk(s["x_q"], t), weights["in"])
 
         def s_stage(g, t):
             s = st[g]

@@ -15,12 +15,10 @@ P = 128
 B = 4096
 H = 512
 TILES = 4
-LOAD = TILES * P
 HALF = 2
 GROUP = HALF * P
 GROUPS = B // GROUP
 LN_EPS = 1e-5
-KB = 6
 TAU_EPS = 1e-6
 
 FLOPS = 3 * 2 * B * H * H
@@ -31,14 +29,14 @@ def tile_advancedliquidneuralnetwork_pb_t_kernel(
 ):
     nc = tc.nc
 
-    def load_rows_view(dram, n):
-        return dram[n * LOAD : (n + 1) * LOAD, :].rearrange("(p t) f -> p t f", t=TILES)
+    def group_rows(dram, g):
+        return dram[g * GROUP : (g + 1) * GROUP, :].rearrange("(p t) f -> p t f", t=HALF)
 
     with ExitStack() as ctx:
         consts = ctx.enter_context(tc.tile_pool(name="consts", bufs=1))
         rows = ctx.enter_context(tc.tile_pool(name="rows", bufs=4))
-        stage = ctx.enter_context(tc.tile_pool(name="stage", bufs=4))
-        codes = ctx.enter_context(tc.tile_pool(name="codes", bufs=4))
+        stage = ctx.enter_context(tc.tile_pool(name="stage", bufs=3))
+        codes = ctx.enter_context(tc.tile_pool(name="codes", bufs=3))
         work = ctx.enter_context(tc.tile_pool(name="work", bufs=2))
         kept = ctx.enter_context(tc.tile_pool(name="kept", bufs=1))
         small = ctx.enter_context(tc.tile_pool(name="small", bufs=6))
@@ -54,7 +52,7 @@ def tile_advancedliquidneuralnetwork_pb_t_kernel(
         make_identity(nc, ident[:])
         ident_bf16 = consts.tile([P, P], BF16)
         make_identity(nc, ident_bf16[:])
-        minus_half = consts.tile([P, HALF], F32)
+        minus_half = consts.tile([P, 4], F32)
         nc.vector.memset(minus_half[:], -0.5)
 
         def bf16_view(grouped):
@@ -89,25 +87,27 @@ def tile_advancedliquidneuralnetwork_pb_t_kernel(
         def chunk(q, i):
             return q[0][:, i * P : (i + 1) * P], q[1][:, i * P : (i + 1) * P]
 
-        def load_weight(view, name):
-            w_sb = consts.tile([P, TILES, H], BF16, name=name + "_sb")
+        def load_weight(view, name, slot):
+            w_sb = kept.tile([P, TILES, H], BF16, name=name + "_sb", tag="out%d" % slot)
             for i in range(2):
                 nc.sync.dma_start(out=w_sb[:, 2 * i : 2 * i + 2, :], in_=view[:, 2 * i : 2 * i + 2, :])
             return w_sb
 
-        def load(name, dram, n):
-            if 0 <= n < B // LOAD:
-                sb = rows.tile([P, TILES, H], BF16, name=name + "_sb", bufs=5 if name == "liq" else 3)
-                nc.sync.dma_start(out=sb[:], in_=load_rows_view(dram, n))
-                loaded[name, n] = sb
+        def load(name, dram, g):
+            if 0 <= g < GROUPS:
+                sb = rows.tile([P, HALF, H], BF16, name=name + "_sb", bufs=DEPTH[name])
+                nc.sync.dma_start(out=sb[:], in_=group_rows(dram, g))
+                loaded[name, g] = sb
 
         loaded = {}
+        DEPTH = {"liq": 9, "x": 5, "h": 4}
         weights = {}
-        weights["v", "sb"] = load_weight(W_v.rearrange("(p j) k -> p j k", j=TILES), "wv")
+        weights["v", "sb"] = load_weight(W_v.rearrange("(p j) k -> p j k", j=TILES), "wv", GROUPS - 1)
         load("liq", liq, 0)
-        weights["o", "sb"] = load_weight(W_o.rearrange("(a p) k -> p a k", p=P), "wo")
         load("liq", liq, 1)
-        weights["in", "sb"] = load_weight(W_in.rearrange("(a p) k -> p a k", p=P), "win")
+        weights["o", "sb"] = load_weight(W_o.rearrange("(a p) k -> p a k", p=P), "wo", GROUPS - 2)
+        load("liq", liq, 2)
+        weights["in", "sb"] = load_weight(W_in.rearrange("(a p) k -> p a k", p=P), "win", GROUPS - 3)
 
         bv_bf16 = consts.tile([P, TILES], BF16)
         nc.scalar.dma_start(out=bv_bf16[:], in_=b_v.rearrange("(p j) -> p j", j=TILES))
@@ -121,7 +121,7 @@ def tile_advancedliquidneuralnetwork_pb_t_kernel(
         def weight_words(name, pair, tag, copy):
             w = weights
             if pair == 0:
-                w[name, "grouped"] = stage.tile([P, H, 2], F32, align_bytes=64, name="w_grouped", bufs=2)
+                w[name, "grouped"] = work.tile([P, H, 2], F32, align_bytes=64, name="w_grouped", tag="gatedT")
             words = psum.tile([P, 2, 2, P], F32, name="w_words", tag=tag, bufs=BUFS[tag])
             turn_words(w[name, "sb"], pair, words)
             words_out(copy, w[name, "grouped"], pair, words)
@@ -169,12 +169,15 @@ def tile_advancedliquidneuralnetwork_pb_t_kernel(
             nc.scalar.copy(out=dst[:], in_=ps[:].rearrange("p j m -> p (j m)"))
 
         st = [{} for g in range(GROUPS)]
+        mean_var = kept.tile([P, GROUPS, 2], F32)
+        sum_sq = kept.tile([P, GROUPS], F32)
+        rstd = kept.tile([P, HALF, GROUPS], F32)
 
         def words_turn(g, name):
             s = st[g]
-            s[name + "T"] = stage.tile([P, GROUP, 2], F32, align_bytes=64, name=name + "T")
+            s[name + "T"] = stage.tile([P, GROUP, 2], F32, align_bytes=64, name="wordsT")
             s["words"] = psum.tile([P, 2, 2, P], F32, name="words", tag="words", bufs=BUFS["words"])
-            turn_words(loaded[name, g // 2], g % 2, s["words"])
+            turn_words(loaded[name, g], 0, s["words"])
 
         def words_copy(g, name):
             words_out(nc.scalar.copy, st[g][name + "T"], 0, st[g]["words"])
@@ -191,9 +194,9 @@ def tile_advancedliquidneuralnetwork_pb_t_kernel(
 
         def v_mx(g, t):
             s = st[g]
-            s["v_acc"] = psum.tile([P, TILES, P], F32, name="v_acc", tag="first", bufs=BUFS["first"])
+            s["v_acc", t] = psum.tile([P, TILES, P], F32, name="v_acc", tag="first", bufs=BUFS["first"])
             for j in range(TILES):
-                mx_pass(s["v_acc"][:, j, :], chunk(weights["v"], j), chunk(s["liq_q"], t))
+                mx_pass(s["v_acc", t][:, j, :], chunk(weights["v"], j), chunk(s["liq_q"], t))
 
         def v_out(g, t):
             s = st[g]
@@ -201,16 +204,16 @@ def tile_advancedliquidneuralnetwork_pb_t_kernel(
                 s["v_bf16"] = stage.tile([P, GROUP, TILES], BF16, align_bytes=64, name="v_bf16")
             nc.vector.tensor_tensor(
                 out=s["v_bf16"][:, t * P : (t + 1) * P, :],
-                in0=s["v_acc"][:].rearrange("p j n -> p n j"),
+                in0=s["v_acc", t][:].rearrange("p j n -> p n j"),
                 in1=bv[:].unsqueeze(1).to_broadcast([P, P, TILES]),
                 op=ALU.add,
             )
 
         def att_mx(g, i):
             s = st[g]
-            s["att"] = psum.tile([P, 2, GROUP], F32, name="att", tag="second", bufs=BUFS["second"])
+            s["att", i] = psum.tile([P, 2, GROUP], F32, name="att", tag="second", bufs=BUFS["second"])
             for jj in range(2):
-                mx_pass(s["att"][:, jj, :], chunk(weights["o"], 2 * i + jj), s["v_q"])
+                mx_pass(s["att", i][:, jj, :], chunk(weights["o"], 2 * i + jj), s["v_q"])
 
         def att_out(g, i):
             s = st[g]
@@ -219,26 +222,24 @@ def tile_advancedliquidneuralnetwork_pb_t_kernel(
             for jj in range(2):
                 j = 2 * i + jj
                 nc.scalar.activation(
-                    out=s["attT"][:, j, :], in_=s["att"][:, jj, :], func=ACT.Identity, bias=cols[:, 0, j : j + 1]
+                    out=s["attT"][:, j, :], in_=s["att", i][:, jj, :], func=ACT.Identity, bias=cols[:, 0, j : j + 1]
                 )
 
-        def u_sum(g, t):
+        def u_open(g, t):
             s = st[g]
-            u = psum.tile([P, H], F32, name="u", tag="turned", bufs=BUFS["turned"])
-            s["u", t] = u
-            nc.tensor.matmul(
-                out=u[:], lhsT=ident_bf16[:], rhs=loaded["liq", g // 2][:, 2 * (g % 2) + t, :], start=True, stop=False
-            )
+            s["u", t] = psum.tile([P, H], F32, name="u", tag="turned", bufs=BUFS["turned"])
+            nc.tensor.matmul(out=s["u", t][:], lhsT=ident_bf16[:], rhs=loaded["liq", g][:, t, :], start=True, stop=False)
+
+        def u_turn(g, t):
+            s = st[g]
             for j in range(TILES):
                 nc.tensor.matmul(
-                    out=u[:, j * P : (j + 1) * P], lhsT=s["attT"][:, j, t * P : (t + 1) * P], rhs=ident[:],
+                    out=s["u", t][:, j * P : (j + 1) * P], lhsT=s["attT"][:, j, t * P : (t + 1) * P], rhs=ident[:],
                     is_transpose=True, start=False, stop=j == TILES - 1,
                 )
 
         def sum_stage(g, t):
             s = st[g]
-            if t == 0:
-                s["var"] = small.tile([P, HALF], F32, name="var")
             if t in BN:
                 return
             s["neg_mean", t] = small.tile([P, 1], F32, name="neg_mean")
@@ -251,11 +252,10 @@ def tile_advancedliquidneuralnetwork_pb_t_kernel(
             s = st[g]
             if t in BN:
                 return
-            s["sum_sq", t] = small.tile([P, 1], F32, name="sum_sq")
             unused = work.tile([P, H], BF16, name="unused")
             nc.scalar.activation(
                 out=unused[:], in_=s["u", t][:], func=ACT.Square, bias=s["neg_mean", t][:],
-                accum_out=s["sum_sq", t][:],
+                accum_out=sum_sq[:, g : g + 1],
             )
 
         def bn_stage(g, t):
@@ -267,20 +267,18 @@ def tile_advancedliquidneuralnetwork_pb_t_kernel(
         def bn_end(g, t):
             s = st[g]
             if t in BN:
-                s["mean_var", t] = small.tile([P, 2], F32, name="mean_var")
-                nc.vector.bn_aggr(out=s["mean_var", t][:], in_=s["stats"][:])
+                nc.vector.bn_aggr(out=mean_var[:, g, :], in_=s["stats"][:])
 
         def rstd_stage(g):
-            s = st[g]
-            r = kept.tile([P, HALF], F32, name="rstd%d" % g)
-            s["rstd"] = r
+            done = slice(g - 3, g + 1)
+            nc.gpsimd.tensor_scalar(
+                out=rstd[:, 0, done], in0=mean_var[:, done, 1], scalar1=1.0, scalar2=LN_EPS, op0=ALU.mult, op1=ALU.add
+            )
+            nc.gpsimd.tensor_scalar(
+                out=rstd[:, 1, done], in0=sum_sq[:, done], scalar1=1.0 / H, scalar2=LN_EPS, op0=ALU.mult, op1=ALU.add
+            )
             for t in range(HALF):
-                src = s["mean_var", t][:, 1:2] if t in BN else s["sum_sq", t][:]
-                nc.gpsimd.tensor_scalar(
-                    out=r[:, t : t + 1], in0=src, scalar1=1.0 if t in BN else 1.0 / H, scalar2=LN_EPS,
-                    op0=ALU.mult, op1=ALU.add,
-                )
-            nc.gpsimd.tensor_tensor(out=r[:], in0=r[:], in1=minus_half[:], op=ALU.pow)
+                nc.gpsimd.tensor_tensor(out=rstd[:, t, done], in0=rstd[:, t, done], in1=minus_half[:], op=ALU.pow)
 
         def w_stage(g, t):
             s = st[g]
@@ -288,150 +286,145 @@ def tile_advancedliquidneuralnetwork_pb_t_kernel(
                 s["w"] = kept.tile([P, HALF, H], F32, name="w%d" % g)
             nc.vector.scalar_tensor_tensor(
                 out=s["w"][:, t, :], in0=s["u", t][:],
-                scalar=s["mean_var", t][:, 0:1] if t in BN else s["neg_mean", t][:],
+                scalar=mean_var[:, g, 0:1] if t in BN else s["neg_mean", t][:],
                 in1=g_all[:], op0=ALU.subtract if t in BN else ALU.add, op1=ALU.mult,
             )
 
         def xin_mx(g, t):
             s = st[g]
-            s["xin"] = psum.tile([P, H], F32, name="xin", tag="first", bufs=BUFS["first"])
-            for again in range(2):
-                mx_pass(s["xin"][:], chunk(s["x_q"], t), weights["in"])
+            s["xin", t] = psum.tile([P, H], F32, name="xin", tag="first", bufs=BUFS["first"])
+            half = slice(0, H // 2)
+            mx_pass(s["xin", t][:, half], chunk(s["x_q"], t), (weights["in"][0][:, half], weights["in"][1][:, half]))
+            mx_pass(s["xin", t][:], chunk(s["x_q"], t), weights["in"])
 
         def s_stage(g, t):
             s = st[g]
             nc.vector.scalar_tensor_tensor(
-                out=s["w"][:, t, :], in0=s["w"][:, t, :], scalar=s["rstd"][:, t : t + 1],
-                in1=s["xin"][:], op0=ALU.mult, op1=ALU.add,
+                out=s["w"][:, t, :], in0=s["w"][:, t, :], scalar=rstd[:, t, g : g + 1],
+                in1=s["xin", t][:], op0=ALU.mult, op1=ALU.add,
             )
 
         def s_turn(g, i):
             s = st[g]
-            s["sT"] = psum.tile([P, 2, HALF, P], F32, name="sT", tag="second", bufs=BUFS["second"])
+            s["sT", i] = psum.tile([P, 2, HALF, P], F32, name="sT", tag="second", bufs=BUFS["second"])
             for jj in range(2):
                 j = 2 * i + jj
                 for t in range(HALF):
                     nc.tensor.transpose(
-                        out=s["sT"][:, jj, t, :], in_=s["w"][:, t, j * P : (j + 1) * P], identity=ident[:]
+                        out=s["sT", i][:, jj, t, :], in_=s["w"][:, t, j * P : (j + 1) * P], identity=ident[:]
                     )
 
         def tanh_stage(g, i):
             s = st[g]
-            s["tanhT"] = work.tile([P, 2, GROUP], F32, name="tanhT")
+            s["tanhT", i] = work.tile([P, 2, GROUP], F32, name="tanhT")
             for jj in range(2):
                 j = 2 * i + jj
                 nc.scalar.activation(
-                    out=s["tanhT"][:, jj, :], in_=s["sT"][:, jj, :, :].rearrange("p t n -> p (t n)"),
+                    out=s["tanhT", i][:, jj, :], in_=s["sT", i][:, jj, :, :].rearrange("p t n -> p (t n)"),
                     func=ACT.Tanh, bias=tanh_bias[:, j : j + 1],
                 )
 
         def gate_stage(g, i):
             s = st[g]
             if i == 0:
-                s["gatedT"] = work.tile([P, TILES, GROUP], F32, name="gatedT")
+                s["gatedT"] = work.tile([P, TILES, GROUP], F32, align_bytes=64, name="gatedT", tag="gatedT")
             for jj in range(2):
                 j = 2 * i + jj
-                nc.scalar.activation(
-                    out=s["gatedT"][:, j, :], in_=s["tanhT"][:, jj, :], func=ACT.Copy, scale=gate[:, j : j + 1]
+                nc.gpsimd.tensor_scalar(
+                    out=s["gatedT"][:, j, :], in0=s["tanhT", i][:, jj, :], scalar1=gate[:, j : j + 1], scalar2=0.0,
+                    op0=ALU.mult, op1=ALU.add,
                 )
+
+        def keep_open(g):
+            s = st[g]
+            s["out"] = kept.tile([P, HALF, H], F32, name="out%d" % g)
+            for t in range(HALF):
+                nc.vector.memset(s["out"][:, t, 0:1], 0.0)
 
         def keep_stage(g, t):
             s = st[g]
-            s["h_kept", t] = kept.tile([P, H], F32, name="h_kept", bufs=KB)
             nc.gpsimd.tensor_tensor(
-                out=s["h_kept", t][:], in0=loaded["h", g // 2][:, 2 * (g % 2) + t, :], in1=keep_all[:], op=ALU.mult
+                out=s["out"][:, t, :], in0=loaded["h", g][:, t, :], in1=keep_all[:], op=ALU.mult
             )
 
         def back_turn(g, t):
             s = st[g]
-            s["back"] = psum.tile([P, H], F32, name="back", tag="turned", bufs=BUFS["turned"])
+            s["back", t] = psum.tile([P, H], F32, name="back", tag="turned", bufs=BUFS["turned"])
             for j in range(TILES):
                 nc.tensor.transpose(
-                    out=s["back"][:, j * P : (j + 1) * P], in_=s["gatedT"][:, j, t * P : (t + 1) * P],
+                    out=s["back", t][:, j * P : (j + 1) * P], in_=s["gatedT"][:, j, t * P : (t + 1) * P],
                     identity=ident[:],
                 )
 
         def out_stage(g, t):
             s = st[g]
-            if t == 0:
-                s["out"] = work.tile([P, HALF, H], F32, name="out_sb")
-            nc.vector.tensor_tensor(out=s["out"][:, t, :], in0=s["back"][:], in1=s["h_kept", t][:], op=ALU.add)
+            nc.vector.tensor_tensor(out=s["out"][:, t, :], in0=s["back", t][:], in1=s["out"][:, t, :], op=ALU.add)
             if t == HALF - 1:
-                first = 2 * (g % 2)
-                nc.sync.dma_start(out=load_rows_view(out, g // 2)[:, first : first + HALF, :], in_=s["out"][:])
+                nc.sync.dma_start(out=group_rows(out, g), in_=s["out"][:])
 
-        def item(k, first):
-            n = k - first
-            return divmod(n, HALF) if 0 <= n < GROUPS * HALF else None
+        def both(stage_fn, g):
+            if 0 <= g < GROUPS:
+                for i in range(HALF):
+                    stage_fn(g, i)
 
-        def run(stage_fn, where):
-            if where is not None:
-                stage_fn(*where)
+        def one(stage_fn, g, *args):
+            if 0 <= g < GROUPS:
+                stage_fn(g, *args)
 
         BN = (0,)
-        X0 = 42
-        H0 = 46
-        V0, ATT0, U0, W0, S0, T0, B0 = 4, 8, 11, 12, 46, 48, 50
-        for k in range(B0 + GROUPS * HALF):
-            a = item(k, 0)
-            b = item(k, X0)
-            words = (0, "liq")
-            if k % TILES == 0 and k > 0:
-                load("liq", liq, k // TILES + 1)
-            if (k - X0 + 6) % TILES == 0:
-                load("x", x, (k - X0 + 6) // TILES)
-            if (k - H0 + 6) % TILES == 0:
-                load("h", h, (k - H0 + 6) // TILES)
-            run(v_mx, item(k, V0))
-            run(att_mx, item(k, ATT0))
-            run(xin_mx, item(k, S0))
+        HG = 4
+        VG, AG, UG, WG = 2, 3, 4, 5
+        XG = GROUPS + 1
+        MG, TG, BG = XG + 2, XG + 3, XG + 5
+        for k in range(GROUPS + BG):
+            load("liq", liq, k + 3)
+            load("h", h, k - HG + 2)
+            load("x", x, k - XG + 3)
+            one(quantise_stage, k - AG, "v")
+            one(quantise_stage, k - 1, "liq")
+            one(keep_open, k - HG)
+            both(v_mx, k - VG)
+            both(att_mx, k - AG)
+            both(xin_mx, k - MG)
+            one(words_turn, k, "liq")
             if k == 0:
-                words_turn(*words)
+                words_copy(0, "liq")
                 weight_words("o", 0, "first", nc.vector.tensor_copy)
                 weight_words("o", 1, "first", nc.scalar.copy)
                 vectors()
-            elif k == 5:
-                weight_words("in", 0, "second", nc.scalar.copy)
-            elif k == 6:
-                weight_words("in", 1, "second", nc.scalar.copy)
-            elif k == 1:
                 spread(cols[:, 4, :], g_all, "second")
-            elif k == 2:
                 spread(keep, keep_all, "second")
-            if a and k > 0 and a[1] == 0:
-                words_turn(a[0], "liq")
-            if b and b[1] == 0:
-                words_turn(b[0], "x")
-            run(u_sum, item(k, U0))
-            run(back_turn, item(k, B0))
-            run(s_turn, item(k, T0))
-            run(sum_stage, item(k, W0))
-            run(att_out, item(k, ATT0))
-            run(squares_stage, item(k, W0))
-            if a and a[1] == 0:
-                words_copy(a[0], "liq")
-            if b and b[1] == 0:
-                words_copy(b[0], "x")
-            run(tanh_stage, item(k, T0))
-            run(gate_stage, item(k, T0))
-            run(bn_stage, item(k, W0))
-            run(s_stage, item(k, S0))
-            run(v_out, item(k, V0))
-            run(bn_end, item(k, W0))
-            run(w_stage, item(k, W0))
-            q = item(k, V0)
-            if q and q[1] == HALF - 1:
-                quantise_stage(q[0], "v")
-            if a and a[1] == 1:
-                quantise_stage(a[0], "liq")
-            if b and b[1] == 1:
-                quantise_stage(b[0], "x")
+            elif k == 2:
+                weight_words("in", 0, "second", nc.scalar.copy)
+                weight_words("in", 1, "second", nc.scalar.copy)
+            one(sum_stage, k - WG, 0)
+            one(sum_stage, k - WG, 1)
+            if k > 0:
+                one(words_copy, k, "liq")
+            both(att_out, k - AG)
+            both(squares_stage, k - WG)
             if k == 1:
                 weight_quantise("o")
-            elif k == 8:
+            elif k == 3:
                 weight_quantise("in")
-            run(out_stage, item(k, B0))
-            r = item(k, W0)
-            if r and r[1] == HALF - 1:
-                rstd_stage(r[0])
-            run(keep_stage, item(k, H0))
+            one(bn_stage, k - WG, 0)
+            one(v_out, k - VG, 0)
+            one(bn_end, k - WG, 0)
+            one(quantise_stage, k - XG - 1, "x")
+            one(w_stage, k - WG, 0)
+            one(v_out, k - VG, 1)
+            one(s_stage, k - MG, 0)
+            one(w_stage, k - WG, 1)
+            one(s_stage, k - MG, 1)
+            both(u_open, k - UG)
+            both(u_turn, k - UG)
+            both(back_turn, k - BG)
+            one(words_turn, k - XG, "x")
+            both(s_turn, k - TG)
+            one(words_copy, k - XG, "x")
+            both(tanh_stage, k - TG)
+            both(out_stage, k - BG)
+            both(keep_stage, k - HG)
+            if (k - WG) % 4 == 3:
+                one(rstd_stage, k - WG)
+            both(gate_stage, k - TG)

@@ -19,6 +19,8 @@ HALF = 2
 GROUP = HALF * P
 GROUPS = B // GROUP
 LN_EPS = 1e-5
+W = H + 2
+OUT = 5
 TAU_EPS = 1e-6
 
 FLOPS = 3 * 2 * B * H * H
@@ -52,8 +54,8 @@ def tile_advancedliquidneuralnetwork_pb_t_kernel(
         make_identity(nc, ident[:])
         ident_bf16 = consts.tile([P, P], BF16)
         make_identity(nc, ident_bf16[:])
-        minus_half = consts.tile([P, 4], F32)
-        nc.vector.memset(minus_half[:], -0.5)
+        minus_half = consts.tile([P, 8, HALF], F32)
+        nc.vector.memset(minus_half[:].rearrange("p g t -> p (g t)"), -0.5)
 
         def bf16_view(grouped):
             return grouped[:].rearrange("p c u -> p (c u)").bitcast(BF16)
@@ -87,8 +89,8 @@ def tile_advancedliquidneuralnetwork_pb_t_kernel(
         def chunk(q, i):
             return q[0][:, i * P : (i + 1) * P], q[1][:, i * P : (i + 1) * P]
 
-        def load_weight(view, name, slot):
-            w_sb = kept.tile([P, TILES, H], BF16, name=name + "_sb", tag="out%d" % slot)
+        def load_weight(view, name):
+            w_sb = work.tile([P, TILES, H], BF16, name=name + "_sb", tag="out", bufs=OUT)
             for i in range(2):
                 nc.sync.dma_start(out=w_sb[:, 2 * i : 2 * i + 2, :], in_=view[:, 2 * i : 2 * i + 2, :])
             return w_sb
@@ -100,14 +102,14 @@ def tile_advancedliquidneuralnetwork_pb_t_kernel(
                 loaded[name, g] = sb
 
         loaded = {}
-        DEPTH = {"liq": 9, "x": 5, "h": 4}
+        DEPTH = {"liq": 10, "x": 5, "h": 4}
         weights = {}
-        weights["v", "sb"] = load_weight(W_v.rearrange("(p j) k -> p j k", j=TILES), "wv", GROUPS - 1)
+        weights["v", "sb"] = load_weight(W_v.rearrange("(p j) k -> p j k", j=TILES), "wv")
         load("liq", liq, 0)
         load("liq", liq, 1)
-        weights["o", "sb"] = load_weight(W_o.rearrange("(a p) k -> p a k", p=P), "wo", GROUPS - 2)
+        weights["o", "sb"] = load_weight(W_o.rearrange("(a p) k -> p a k", p=P), "wo")
         load("liq", liq, 2)
-        weights["in", "sb"] = load_weight(W_in.rearrange("(a p) k -> p a k", p=P), "win", GROUPS - 3)
+        weights["in", "sb"] = load_weight(W_in.rearrange("(a p) k -> p a k", p=P), "win")
 
         bv_bf16 = consts.tile([P, TILES], BF16)
         nc.scalar.dma_start(out=bv_bf16[:], in_=b_v.rearrange("(p j) -> p j", j=TILES))
@@ -134,8 +136,8 @@ def tile_advancedliquidneuralnetwork_pb_t_kernel(
             weights[name] = (q[0][:], q[1][:])
             quantise(bf16_view(weights[name, "grouped"]), weights[name])
 
-        weight_words("v", 0, "turned", nc.scalar.copy)
-        weight_words("v", 1, "turned", nc.vector.tensor_copy)
+        weight_words("v", 0, "first", nc.scalar.copy)
+        weight_words("v", 1, "first", nc.vector.tensor_copy)
         weight_quantise("v")
         bv = consts.tile([P, TILES], F32)
         nc.vector.tensor_copy(out=bv[:], in_=bv_bf16[:])
@@ -144,7 +146,8 @@ def tile_advancedliquidneuralnetwork_pb_t_kernel(
         tanh_bias = consts.tile([P, TILES], F32)
         gate = consts.tile([P, TILES], F32)
         keep = consts.tile([P, TILES], F32)
-        g_all = consts.tile([P, H], F32)
+        minus_g = consts.tile([P, W], F32)
+        nc.vector.memset(minus_g[:, H:W], 0.0)
         keep_all = consts.tile([P, H], F32)
 
         def vectors():
@@ -160,27 +163,28 @@ def tile_advancedliquidneuralnetwork_pb_t_kernel(
                 out=keep[:], in0=gate[:], scalar1=-1.0, scalar2=1.0, op0=ALU.mult, op1=ALU.add
             )
 
-        def spread(column, dst, tag):
-            ps = psum.tile([P, TILES, P], F32, name="spread", tag=tag)
+        def spread(column, dst, tag, factor):
+            ps = psum.tile([P, TILES, P], F32, name="spread", tag=tag, bufs=BUFS[tag])
             for j in range(TILES):
                 nc.tensor.transpose(
                     out=ps[:, j, :], in_=column[:, j : j + 1].to_broadcast([P, P]), identity=ident[:]
                 )
-            nc.scalar.copy(out=dst[:], in_=ps[:].rearrange("p j m -> p (j m)"))
+            nc.scalar.mul(out=dst[:, 0:H], in_=ps[:].rearrange("p j m -> p (j m)"), mul=factor)
 
         st = [{} for g in range(GROUPS)]
-        mean_var = kept.tile([P, GROUPS, 2], F32)
-        sum_sq = kept.tile([P, GROUPS], F32)
-        rstd = kept.tile([P, HALF, GROUPS], F32)
+        mean_var = kept.tile([P, GROUPS, HALF, 2], F32)
+        rstd = kept.tile([P, GROUPS, HALF], F32)
 
         def words_turn(g, name):
             s = st[g]
             s[name + "T"] = stage.tile([P, GROUP, 2], F32, align_bytes=64, name="wordsT")
-            s["words"] = psum.tile([P, 2, 2, P], F32, name="words", tag="words", bufs=BUFS["words"])
+            tag = "turned" if name == "liq" and g < 3 else "words"
+            s["words"] = psum.tile([P, 2, 2, P], F32, name="words", tag=tag, bufs=BUFS[tag])
             turn_words(loaded[name, g], 0, s["words"])
 
         def words_copy(g, name):
-            words_out(nc.scalar.copy, st[g][name + "T"], 0, st[g]["words"])
+            copy = nc.vector.tensor_copy if name == "liq" and g == 1 else nc.scalar.copy
+            words_out(copy, st[g][name + "T"], 0, st[g]["words"])
 
         def quantise_stage(g, name):
             s = st[g]
@@ -238,57 +242,37 @@ def tile_advancedliquidneuralnetwork_pb_t_kernel(
                     is_transpose=True, start=False, stop=j == TILES - 1,
                 )
 
-        def sum_stage(g, t):
-            s = st[g]
-            if t in BN:
-                return
-            s["neg_mean", t] = small.tile([P, 1], F32, name="neg_mean")
-            unused = work.tile([P, H], BF16, name="unused")
-            nc.scalar.activation(
-                out=unused[:], in_=s["u", t][:], func=ACT.Copy, scale=-1.0 / H, accum_out=s["neg_mean", t][:]
-            )
-
-        def squares_stage(g, t):
-            s = st[g]
-            if t in BN:
-                return
-            unused = work.tile([P, H], BF16, name="unused")
-            nc.scalar.activation(
-                out=unused[:], in_=s["u", t][:], func=ACT.Square, bias=s["neg_mean", t][:],
-                accum_out=sum_sq[:, g : g + 1],
-            )
-
         def bn_stage(g, t):
             s = st[g]
-            if t in BN:
-                s["stats"] = small.tile([P, 6], F32, name="stats")
-                nc.vector.bn_stats(out=s["stats"][:], in_=s["u", t][:])
+            s["stats", t] = small.tile([P, 6], F32, name="stats")
+            nc.vector.bn_stats(out=s["stats", t][:], in_=s["u", t][:])
 
         def bn_end(g, t):
-            s = st[g]
-            if t in BN:
-                nc.vector.bn_aggr(out=mean_var[:, g, :], in_=s["stats"][:])
+            nc.vector.bn_aggr(out=mean_var[:, g, t, :], in_=st[g]["stats", t][:])
 
-        def rstd_stage(g):
-            done = slice(g - 3, g + 1)
+        def rstd_stage(g0, g1):
             nc.gpsimd.tensor_scalar(
-                out=rstd[:, 0, done], in0=mean_var[:, done, 1], scalar1=1.0, scalar2=LN_EPS, op0=ALU.mult, op1=ALU.add
+                out=rstd[:, g0:g1, :], in0=mean_var[:, g0:g1, :, 1], scalar1=1.0, scalar2=LN_EPS,
+                op0=ALU.mult, op1=ALU.add,
             )
-            nc.gpsimd.tensor_scalar(
-                out=rstd[:, 1, done], in0=sum_sq[:, done], scalar1=1.0 / H, scalar2=LN_EPS, op0=ALU.mult, op1=ALU.add
+            nc.gpsimd.tensor_tensor(
+                out=rstd[:, g0:g1, :], in0=rstd[:, g0:g1, :], in1=minus_half[:, 0 : g1 - g0, :], op=ALU.pow
             )
-            for t in range(HALF):
-                nc.gpsimd.tensor_tensor(out=rstd[:, t, done], in0=rstd[:, t, done], in1=minus_half[:], op=ALU.pow)
 
-        def w_stage(g, t):
+        def centre(g, t):
             s = st[g]
             if t == 0:
-                s["w"] = kept.tile([P, HALF, H], F32, name="w%d" % g)
-            nc.vector.scalar_tensor_tensor(
-                out=s["w"][:, t, :], in0=s["u", t][:],
-                scalar=mean_var[:, g, 0:1] if t in BN else s["neg_mean", t][:],
-                in1=g_all[:], op0=ALU.subtract if t in BN else ALU.add, op1=ALU.mult,
+                s["w"] = kept.tile([P, HALF, W], F32, name="w%d" % g)
+            nc.scalar.activation(
+                out=s["w"][:, t, 0:H], in_=s["u", t][:], func=ACT.Identity, scale=-1.0, bias=mean_var[:, g, t, 0:1]
             )
+
+        def gain_open(g):
+            nc.vector.memset(st[g]["w"][:, :, H:W], 0.0)
+
+        def gain_stage(g, t):
+            w = st[g]["w"]
+            nc.gpsimd.tensor_tensor(out=w[:, t, :], in0=w[:, t, :], in1=minus_g[:], op=ALU.mult)
 
         def xin_mx(g, t):
             s = st[g]
@@ -300,7 +284,7 @@ def tile_advancedliquidneuralnetwork_pb_t_kernel(
         def s_stage(g, t):
             s = st[g]
             nc.vector.scalar_tensor_tensor(
-                out=s["w"][:, t, :], in0=s["w"][:, t, :], scalar=rstd[:, t, g : g + 1],
+                out=s["w"][:, t, 0:H], in0=s["w"][:, t, 0:H], scalar=rstd[:, g, t : t + 1],
                 in1=s["xin", t][:], op0=ALU.mult, op1=ALU.add,
             )
 
@@ -330,16 +314,14 @@ def tile_advancedliquidneuralnetwork_pb_t_kernel(
                 s["gatedT"] = work.tile([P, TILES, GROUP], F32, align_bytes=64, name="gatedT", tag="gatedT")
             for jj in range(2):
                 j = 2 * i + jj
-                nc.gpsimd.tensor_scalar(
-                    out=s["gatedT"][:, j, :], in0=s["tanhT", i][:, jj, :], scalar1=gate[:, j : j + 1], scalar2=0.0,
-                    op0=ALU.mult, op1=ALU.add,
+                nc.scalar.activation(
+                    out=s["gatedT"][:, j, :], in_=s["tanhT", i][:, jj, :], func=ACT.Copy, scale=gate[:, j : j + 1]
                 )
 
         def keep_open(g):
             s = st[g]
-            s["out"] = kept.tile([P, HALF, H], F32, name="out%d" % g)
-            for t in range(HALF):
-                nc.vector.memset(s["out"][:, t, 0:1], 0.0)
+            s["out"] = work.tile([P, HALF, H], F32, name="out", bufs=OUT)
+            nc.vector.memset(s["out"][:, :, 0:1], 0.0)
 
         def keep_stage(g, t):
             s = st[g]
@@ -371,60 +353,59 @@ def tile_advancedliquidneuralnetwork_pb_t_kernel(
             if 0 <= g < GROUPS:
                 stage_fn(g, *args)
 
-        BN = (0,)
-        HG = 4
-        VG, AG, UG, WG = 2, 3, 4, 5
+        VG, AG, UG, WG, GG = 3, 4, 5, 6, 8
         XG = GROUPS + 1
-        MG, TG, BG = XG + 2, XG + 3, XG + 5
+        MG, TG, BG = XG + 3, XG + 4, XG + 6
+        HG = BG - 3
         for k in range(GROUPS + BG):
             load("liq", liq, k + 3)
             load("h", h, k - HG + 2)
             load("x", x, k - XG + 3)
-            one(quantise_stage, k - AG, "v")
-            one(quantise_stage, k - 1, "liq")
+            one(quantise_stage, k - 2, "liq")
+            one(quantise_stage, k - XG - 2, "x")
+            one(gain_open, k - GG)
             one(keep_open, k - HG)
+            one(quantise_stage, k - AG, "v")
             both(v_mx, k - VG)
             both(att_mx, k - AG)
             both(xin_mx, k - MG)
             one(words_turn, k, "liq")
-            if k == 0:
-                words_copy(0, "liq")
-                weight_words("o", 0, "first", nc.vector.tensor_copy)
-                weight_words("o", 1, "first", nc.scalar.copy)
-                vectors()
-                spread(cols[:, 4, :], g_all, "second")
-                spread(keep, keep_all, "second")
-            elif k == 2:
-                weight_words("in", 0, "second", nc.scalar.copy)
-                weight_words("in", 1, "second", nc.scalar.copy)
-            one(sum_stage, k - WG, 0)
-            one(sum_stage, k - WG, 1)
-            if k > 0:
+            if k < 3:
                 one(words_copy, k, "liq")
-            both(att_out, k - AG)
-            both(squares_stage, k - WG)
             if k == 1:
+                weight_words("o", 0, "second", nc.vector.tensor_copy)
+                weight_words("o", 1, "second", nc.scalar.copy)
+            elif k == 2:
+                vectors()
                 weight_quantise("o")
             elif k == 3:
+                spread(cols[:, 4, :], minus_g, "turned", -1.0)
+                spread(keep, keep_all, "turned", 1.0)
+            elif k == XG - 1:
+                weight_words("in", 0, "words", nc.scalar.copy)
+            elif k == XG:
+                weight_words("in", 1, "words", nc.scalar.copy)
+            elif k == XG + 1:
                 weight_quantise("in")
-            one(bn_stage, k - WG, 0)
-            one(v_out, k - VG, 0)
-            one(bn_end, k - WG, 0)
-            one(quantise_stage, k - XG - 1, "x")
-            one(w_stage, k - WG, 0)
-            one(v_out, k - VG, 1)
-            one(s_stage, k - MG, 0)
-            one(w_stage, k - WG, 1)
-            one(s_stage, k - MG, 1)
-            both(u_open, k - UG)
-            both(u_turn, k - UG)
+            both(bn_stage, k - WG)
+            both(bn_end, k - WG)
+            both(centre, k - WG)
+            if k >= 3:
+                one(words_copy, k, "liq")
+            both(att_out, k - AG)
+            both(v_out, k - VG)
+            both(s_stage, k - MG)
+            for t in range(HALF):
+                one(u_open, k - UG, t)
+                one(u_turn, k - UG, t)
             both(back_turn, k - BG)
             one(words_turn, k - XG, "x")
             both(s_turn, k - TG)
             one(words_copy, k - XG, "x")
             both(tanh_stage, k - TG)
             both(out_stage, k - BG)
+            both(gain_stage, k - GG)
             both(keep_stage, k - HG)
-            if (k - WG) % 4 == 3:
-                one(rstd_stage, k - WG)
+            if k - WG in (7, 15):
+                rstd_stage(k - WG - 7, k - WG + 1)
             both(gate_stage, k - TG)

@@ -20,7 +20,7 @@ GROUP = HALF * P
 GROUPS = B // GROUP
 LN_EPS = 1e-5
 W = H + 2
-OUT = 5
+OUT = 10
 TAU_EPS = 1e-6
 
 FLOPS = 3 * 2 * B * H * H
@@ -177,8 +177,8 @@ def tile_advancedliquidneuralnetwork_pb_t_kernel(
 
         def words_turn(g, name):
             s = st[g]
-            s[name + "T"] = stage.tile([P, GROUP, 2], F32, align_bytes=64, name="wordsT")
-            tag = "turned" if name == "liq" and g < 3 else "words"
+            s[name + "T"] = stage.tile([P, GROUP, 2], F32, align_bytes=64, name="wordsT", bufs=5)
+            tag = "turned" if g < 3 and (name == "liq" or EARLY_X) else "words"
             s["words"] = psum.tile([P, 2, 2, P], F32, name="words", tag=tag, bufs=BUFS[tag])
             turn_words(loaded[name, g], 0, s["words"])
 
@@ -189,8 +189,8 @@ def tile_advancedliquidneuralnetwork_pb_t_kernel(
         def quantise_stage(g, name):
             s = st[g]
             q = (
-                codes.tile([P, GROUP], U32, align_bytes=64, name=name + "_words"),
-                codes.tile([P, GROUP], U8, align_bytes=64, name=name + "_scales"),
+                codes.tile([P, GROUP], U32, align_bytes=64, name=name + "_words", bufs=6 if name == "x" else 3),
+                codes.tile([P, GROUP], U8, align_bytes=64, name=name + "_scales", bufs=6 if name == "x" else 3),
             )
             s[name + "_q"] = (q[0][:], q[1][:])
             src = s["v_bf16"][:].rearrange("p n j -> p (n j)") if name == "v" else bf16_view(s[name + "T"])
@@ -341,7 +341,9 @@ def tile_advancedliquidneuralnetwork_pb_t_kernel(
         def out_stage(g, t):
             s = st[g]
             nc.vector.tensor_tensor(out=s["out"][:, t, :], in0=s["back", t][:], in1=s["out"][:, t, :], op=ALU.add)
-            if t == HALF - 1:
+            if g == GROUPS - 1:
+                nc.sync.dma_start(out=group_rows(out, g)[:, t, :], in_=s["out"][:, t, :])
+            elif t == HALF - 1:
                 nc.sync.dma_start(out=group_rows(out, g), in_=s["out"][:])
 
         def both(stage_fn, g):
@@ -353,25 +355,31 @@ def tile_advancedliquidneuralnetwork_pb_t_kernel(
             if 0 <= g < GROUPS:
                 stage_fn(g, *args)
 
-        VG, AG, UG, WG, GG = 3, 4, 5, 6, 8
+        VG, AG, UG, WG, GG = 3, 4, 5, 6, 7
         XG = GROUPS + 1
         MG, TG, BG = XG + 3, XG + 4, XG + 6
-        HG = BG - 3
+        EARLY_X = 0
+        WI = XG - 2
+        keep_at = {3 + g if g < 3 else BG + g - 3: g for g in range(GROUPS)}
+        x_at = {2 + g if g < 0 else XG + g: g for g in range(GROUPS)}
         for k in range(GROUPS + BG):
             load("liq", liq, k + 3)
-            load("h", h, k - HG + 2)
-            load("x", x, k - XG + 3)
-            one(quantise_stage, k - 2, "liq")
-            one(quantise_stage, k - XG - 2, "x")
-            one(gain_open, k - GG)
-            one(keep_open, k - HG)
+            load("h", h, keep_at.get(k + 2, -1))
+            load("x", x, x_at.get(k + 2, -1))
+            if k > 2:
+                one(quantise_stage, k - 2, "liq")
+            one(quantise_stage, x_at.get(k - 2, -1), "x")
             one(quantise_stage, k - AG, "v")
+            one(gain_open, k - GG)
+            one(keep_open, keep_at.get(k, -1))
             both(v_mx, k - VG)
             both(att_mx, k - AG)
             both(xin_mx, k - MG)
             one(words_turn, k, "liq")
             if k < 3:
                 one(words_copy, k, "liq")
+                if k == 0:
+                    quantise_stage(0, "liq")
             if k == 1:
                 weight_words("o", 0, "second", nc.vector.tensor_copy)
                 weight_words("o", 1, "second", nc.scalar.copy)
@@ -381,11 +389,11 @@ def tile_advancedliquidneuralnetwork_pb_t_kernel(
             elif k == 3:
                 spread(cols[:, 4, :], minus_g, "turned", -1.0)
                 spread(keep, keep_all, "turned", 1.0)
-            elif k == XG - 1:
-                weight_words("in", 0, "words", nc.scalar.copy)
-            elif k == XG:
-                weight_words("in", 1, "words", nc.scalar.copy)
-            elif k == XG + 1:
+            elif k == WI:
+                weight_words("in", 0, "turned", nc.scalar.copy)
+            elif k == WI + 1:
+                weight_words("in", 1, "turned", nc.scalar.copy)
+            elif k == WI + 2:
                 weight_quantise("in")
             both(bn_stage, k - WG)
             both(bn_end, k - WG)
@@ -399,13 +407,13 @@ def tile_advancedliquidneuralnetwork_pb_t_kernel(
                 one(u_open, k - UG, t)
                 one(u_turn, k - UG, t)
             both(back_turn, k - BG)
-            one(words_turn, k - XG, "x")
+            one(words_turn, x_at.get(k, -1), "x")
             both(s_turn, k - TG)
-            one(words_copy, k - XG, "x")
+            one(words_copy, x_at.get(k, -1), "x")
             both(tanh_stage, k - TG)
             both(out_stage, k - BG)
             both(gain_stage, k - GG)
-            both(keep_stage, k - HG)
+            both(keep_stage, keep_at.get(k, -1))
             if k - WG in (7, 15):
                 rstd_stage(k - WG - 7, k - WG + 1)
             both(gate_stage, k - TG)

@@ -102,6 +102,7 @@ def tile_advancedliquidneuralnetwork_pb_t_kernel(
                 loaded[name, g] = sb
 
         loaded = {}
+        LAST = 14
         DEPTH = {"liq": 10, "x": 5, "h": 4}
         weights = {}
         weights["v", "sb"] = load_weight(W_v.rearrange("(p j) k -> p j k", j=TILES), "wv")
@@ -277,8 +278,6 @@ def tile_advancedliquidneuralnetwork_pb_t_kernel(
         def xin_mx(g, t):
             s = st[g]
             s["xin", t] = psum.tile([P, H], F32, name="xin", tag="first", bufs=BUFS["first"])
-            half = slice(0, H // 2)
-            mx_pass(s["xin", t][:, half], chunk(s["x_q"], t), (weights["in"][0][:, half], weights["in"][1][:, half]))
             mx_pass(s["xin", t][:], chunk(s["x_q"], t), weights["in"])
 
         def s_stage(g, t):
@@ -314,9 +313,14 @@ def tile_advancedliquidneuralnetwork_pb_t_kernel(
                 s["gatedT"] = work.tile([P, TILES, GROUP], F32, align_bytes=64, name="gatedT", tag="gatedT")
             for jj in range(2):
                 j = 2 * i + jj
-                nc.scalar.activation(
-                    out=s["gatedT"][:, j, :], in_=s["tanhT", i][:, jj, :], func=ACT.Copy, scale=gate[:, j : j + 1]
-                )
+                if g >= LAST and jj == 1:
+                    nc.vector.tensor_scalar_mul(
+                        out=s["gatedT"][:, j, :], in0=s["tanhT", i][:, jj, :], scalar1=gate[:, j : j + 1]
+                    )
+                else:
+                    nc.scalar.activation(
+                        out=s["gatedT"][:, j, :], in_=s["tanhT", i][:, jj, :], func=ACT.Copy, scale=gate[:, j : j + 1]
+                    )
 
         def keep_open(g):
             s = st[g]
@@ -359,7 +363,7 @@ def tile_advancedliquidneuralnetwork_pb_t_kernel(
         XG = GROUPS + 1
         MG, TG, BG = XG + 3, XG + 4, XG + 6
         EARLY_X = 0
-        WI = XG - 2
+        WI = XG - 13
         keep_at = {3 + g if g < 3 else BG + g - 3: g for g in range(GROUPS)}
         x_at = {2 + g if g < 0 else XG + g: g for g in range(GROUPS)}
         for k in range(GROUPS + BG):
@@ -368,10 +372,10 @@ def tile_advancedliquidneuralnetwork_pb_t_kernel(
             load("x", x, x_at.get(k + 2, -1))
             if k > 2:
                 one(quantise_stage, k - 2, "liq")
-            one(quantise_stage, x_at.get(k - 2, -1), "x")
             one(quantise_stage, k - AG, "v")
             one(gain_open, k - GG)
             one(keep_open, keep_at.get(k, -1))
+            one(quantise_stage, x_at.get(k - 2, -1), "x")
             both(v_mx, k - VG)
             both(att_mx, k - AG)
             both(xin_mx, k - MG)
@@ -396,12 +400,15 @@ def tile_advancedliquidneuralnetwork_pb_t_kernel(
             elif k == WI + 2:
                 weight_quantise("in")
             both(bn_stage, k - WG)
-            both(bn_end, k - WG)
-            both(centre, k - WG)
+            one(bn_end, k - WG, 0)
+            one(centre, k - WG, 0)
+            one(v_out, k - VG, 0)
+            one(bn_end, k - WG, 1)
+            one(centre, k - WG, 1)
+            one(v_out, k - VG, 1)
+            both(att_out, k - AG)
             if k >= 3:
                 one(words_copy, k, "liq")
-            both(att_out, k - AG)
-            both(v_out, k - VG)
             both(s_stage, k - MG)
             for t in range(HALF):
                 one(u_open, k - UG, t)

@@ -278,6 +278,8 @@ def tile_advancedliquidneuralnetwork_pb_t_kernel(
         def xin_mx(g, t):
             s = st[g]
             s["xin", t] = psum.tile([P, H], F32, name="xin", tag="first", bufs=BUFS["first"])
+            half = slice(0, H // 2)
+            mx_pass(s["xin", t][:, half], chunk(s["x_q"], t), (weights["in"][0][:, half], weights["in"][1][:, half]))
             mx_pass(s["xin", t][:], chunk(s["x_q"], t), weights["in"])
 
         def s_stage(g, t):
@@ -372,10 +374,13 @@ def tile_advancedliquidneuralnetwork_pb_t_kernel(
             load("x", x, x_at.get(k + 2, -1))
             if k > 2:
                 one(quantise_stage, k - 2, "liq")
+            if k - GG < GROUPS:
+                one(quantise_stage, x_at.get(k - 2, -1), "x")
             one(quantise_stage, k - AG, "v")
             one(gain_open, k - GG)
             one(keep_open, keep_at.get(k, -1))
-            one(quantise_stage, x_at.get(k - 2, -1), "x")
+            if k - GG >= GROUPS:
+                one(quantise_stage, x_at.get(k - 2, -1), "x")
             both(v_mx, k - VG)
             both(att_mx, k - AG)
             both(xin_mx, k - MG)
@@ -397,7 +402,7 @@ def tile_advancedliquidneuralnetwork_pb_t_kernel(
                 weight_words("in", 0, "turned", nc.scalar.copy)
             elif k == WI + 1:
                 weight_words("in", 1, "turned", nc.scalar.copy)
-            elif k == WI + 2:
+            elif k == WI + 3:
                 weight_quantise("in")
             both(bn_stage, k - WG)
             one(bn_end, k - WG, 0)

@@ -226,9 +226,14 @@ def tile_advancedliquidneuralnetwork_pb_t_kernel(
                 s["attT"] = work.tile([P, TILES, GROUP], F32, name="attT")
             for jj in range(2):
                 j = 2 * i + jj
-                nc.scalar.activation(
-                    out=s["attT"][:, j, :], in_=s["att", i][:, jj, :], func=ACT.Identity, bias=cols[:, 0, j : j + 1]
-                )
+                if g < 2 and jj == 1:
+                    nc.vector.tensor_scalar_add(
+                        out=s["attT"][:, j, :], in0=s["att", i][:, jj, :], scalar1=cols[:, 0, j : j + 1]
+                    )
+                else:
+                    nc.scalar.activation(
+                        out=s["attT"][:, j, :], in_=s["att", i][:, jj, :], func=ACT.Identity, bias=cols[:, 0, j : j + 1]
+                    )
 
         def u_open(g, t):
             s = st[g]
@@ -365,7 +370,7 @@ def tile_advancedliquidneuralnetwork_pb_t_kernel(
         XG = GROUPS + 1
         MG, TG, BG = XG + 3, XG + 4, XG + 6
         EARLY_X = 0
-        WI = XG - 13
+        WI = XG - 14
         keep_at = {3 + g if g < 3 else BG + g - 3: g for g in range(GROUPS)}
         x_at = {2 + g if g < 0 else XG + g: g for g in range(GROUPS)}
         for k in range(GROUPS + BG):
@@ -376,14 +381,15 @@ def tile_advancedliquidneuralnetwork_pb_t_kernel(
                 one(quantise_stage, k - 2, "liq")
             if k - GG < GROUPS:
                 one(quantise_stage, x_at.get(k - 2, -1), "x")
-            one(quantise_stage, k - AG, "v")
             one(gain_open, k - GG)
+            one(quantise_stage, k - AG, "v")
             one(keep_open, keep_at.get(k, -1))
             if k - GG >= GROUPS:
                 one(quantise_stage, x_at.get(k - 2, -1), "x")
             both(v_mx, k - VG)
             both(att_mx, k - AG)
             both(xin_mx, k - MG)
+            one(u_open, k - UG, 0)
             one(words_turn, k, "liq")
             if k < 3:
                 one(words_copy, k, "liq")
@@ -398,11 +404,11 @@ def tile_advancedliquidneuralnetwork_pb_t_kernel(
             elif k == 3:
                 spread(cols[:, 4, :], minus_g, "turned", -1.0)
                 spread(keep, keep_all, "turned", 1.0)
-            elif k == WI:
+            if k == WI:
                 weight_words("in", 0, "turned", nc.scalar.copy)
             elif k == WI + 1:
                 weight_words("in", 1, "turned", nc.scalar.copy)
-            elif k == WI + 3:
+            elif k == WI + 4:
                 weight_quantise("in")
             both(bn_stage, k - WG)
             one(bn_end, k - WG, 0)
@@ -415,9 +421,9 @@ def tile_advancedliquidneuralnetwork_pb_t_kernel(
             if k >= 3:
                 one(words_copy, k, "liq")
             both(s_stage, k - MG)
-            for t in range(HALF):
-                one(u_open, k - UG, t)
-                one(u_turn, k - UG, t)
+            one(u_turn, k - UG, 0)
+            one(u_open, k - UG, 1)
+            one(u_turn, k - UG, 1)
             both(back_turn, k - BG)
             one(words_turn, x_at.get(k, -1), "x")
             both(s_turn, k - TG)

from contextlib import ExitStack

import concourse.mybir as mybir
from concourse.masks import make_identity

F32 = mybir.dt.float32
BF16 = mybir.dt.bfloat16
U32 = mybir.dt.uint32
U8 = mybir.dt.uint8
FP8X4 = mybir.dt.float8_e4m3fn_x4
ALU = mybir.AluOpType
ACT = mybir.ActivationFunctionType

P = 128
B = 4096
H = 512
TILES = 4
HALF = 2
GROUP = HALF * P
GROUPS = B // GROUP
LN_EPS = 1e-5
W = H + 2
OUT = 10
TAU_EPS = 1e-6

FLOPS = 3 * 2 * B * H * H


def tile_advancedliquidneuralnetwork_pb_t_kernel(
    tc, liq, h, x, W_in, b_in, W_v, b_v, W_o, b_o, g_att, beta_att, tau, out
):
    nc = tc.nc

    def group_rows(dram, g):
        return dram[g * GROUP : (g + 1) * GROUP, :].rearrange("(p t) f -> p t f", t=HALF)

    with ExitStack() as ctx:
        consts = ctx.enter_context(tc.tile_pool(name="consts", bufs=1))
        rows = ctx.enter_context(tc.tile_pool(name="rows", bufs=4))
        stage = ctx.enter_context(tc.tile_pool(name="stage", bufs=3))
        codes = ctx.enter_context(tc.tile_pool(name="codes", bufs=3))
        work = ctx.enter_context(tc.tile_pool(name="work", bufs=2))
        kept = ctx.enter_context(tc.tile_pool(name="kept", bufs=1))
        small = ctx.enter_context(tc.tile_pool(name="small", bufs=6))
        psum = ctx.enter_context(tc.psum_pool(name="psum", bufs=2))
        BUFS = {"words": 1, "first": 2, "second": 2, "turned": 3}
        ctx.enter_context(tc.manual_schedule())

        warm = consts.tile([P, 1], F32)
        nc.vector.memset(warm[:], 0.0)
        nc.scalar.activation(out=warm[:], in_=warm[:], func=ACT.Tanh)

        ident = consts.tile([P, P], F32)
        make_identity(nc, ident[:])
        ident_bf16 = consts.tile([P, P], BF16)
        make_identity(nc, ident_bf16[:])
        minus_half = consts.tile([P, 8, HALF], F32)
        nc.vector.memset(minus_half[:].rearrange("p g t -> p (g t)"), -0.5)

        def bf16_view(grouped):
            return grouped[:].rearrange("p c u -> p (c u)").bitcast(BF16)

        def turn_words(src, pair, words):
            for i in range(2):
                view = src[:, 2 * pair + i, :].bitcast(F32).rearrange("r (p u) -> r u p", u=2)
                for u in range(2):
                    nc.tensor.transpose(out=words[:, i, u, :], in_=view[:, u, :], identity=ident[:])

        def words_out(copy, grouped, pair, words):
            copy(
                out=grouped[:, 2 * pair * P : 2 * (pair + 1) * P, :].rearrange("p (i c) u -> p i c u", i=2),
                in_=words[:].rearrange("p i u c -> p i c u"),
            )

        def quantise(grouped_bf16, q):
            nc.vector.quantize_mx(out=q[0].bitcast(FP8X4), scales=q[1], in_=grouped_bf16)

        def mx_pass(acc, stationary, moving):
            nc.tensor.matmul_mx(
                out=acc,
                lhsT=stationary[0].bitcast(FP8X4),
                lhsT_scale=stationary[1],
                rhs=moving[0].bitcast(FP8X4),
                rhs_scale=moving[1],
                start=True,
                stop=True,
            )

        def chunk(q, i):
            return q[0][:, i * P : (i + 1) * P], q[1][:, i * P : (i + 1) * P]

        def load_weight(view, name):
            w_sb = work.tile([P, TILES, H], BF16, name=name + "_sb", tag="out", bufs=OUT)
            for i in range(2):
                nc.sync.dma_start(out=w_sb[:, 2 * i : 2 * i + 2, :], in_=view[:, 2 * i : 2 * i + 2, :])
            return w_sb

        def load(name, dram, g):
            if 0 <= g < GROUPS:
                sb = rows.tile([P, HALF, H], BF16, name=name + "_sb", bufs=DEPTH[name])
                nc.sync.dma_start(out=sb[:], in_=group_rows(dram, g))
                loaded[name, g] = sb

        loaded = {}
        LAST = 14
        DEPTH = {"liq": 10, "x": 5, "h": 4}
        weights = {}
        weights["v", "sb"] = load_weight(W_v.rearrange("(p j) k -> p j k", j=TILES), "wv")
        load("liq", liq, 0)
        load("liq", liq, 1)
        weights["o", "sb"] = load_weight(W_o.rearrange("(a p) k -> p a k", p=P), "wo")
        load("liq", liq, 2)
        weights["in", "sb"] = load_weight(W_in.rearrange("(a p) k -> p a k", p=P), "win")

        bv_bf16 = consts.tile([P, TILES], BF16)
        nc.scalar.dma_start(out=bv_bf16[:], in_=b_v.rearrange("(p j) -> p j", j=TILES))
        vec_rows = consts.tile([P, P], BF16)
        nc.vector.memset(vec_rows[:], 0.0)
        for n, vec in enumerate((b_o, b_in, beta_att, tau, g_att)):
            nc.scalar.dma_start(
                out=vec_rows[n * TILES : (n + 1) * TILES, :], in_=vec.rearrange("(j p) -> j p", p=P)
            )

        def weight_words(name, pair, tag, copy):
            w = weights
            if pair == 0:
                w[name, "grouped"] = work.tile([P, H, 2], F32, align_bytes=64, name="w_grouped", tag="gatedT")
            words = psum.tile([P, 2, 2, P], F32, name="w_words", tag=tag, bufs=BUFS[tag])
            turn_words(w[name, "sb"], pair, words)
            words_out(copy, w[name, "grouped"], pair, words)

        def weight_quantise(name):
            q = (
                consts.tile([P, H], U32, align_bytes=64, name="w" + name + "_words"),
                consts.tile([P, H], U8, align_bytes=64, name="w" + name + "_scales"),
            )
            weights[name] = (q[0][:], q[1][:])
            quantise(bf16_view(weights[name, "grouped"]), weights[name])

        weight_words("v", 0, "first", nc.scalar.copy)
        weight_words("v", 1, "first", nc.vector.tensor_copy)
        weight_quantise("v")
        bv = consts.tile([P, TILES], F32)
        nc.vector.tensor_copy(out=bv[:], in_=bv_bf16[:])

        cols = consts.tile([P, 5, TILES], F32)
        tanh_bias = consts.tile([P, TILES], F32)
        gate = consts.tile([P, TILES], F32)
        keep = consts.tile([P, TILES], F32)
        minus_g = consts.tile([P, W], F32)
        nc.vector.memset(minus_g[:, H:W], 0.0)
        keep_all = consts.tile([P, H], F32)

        def vectors():
            vec_ps = psum.tile([P, P], BF16, name="vec_ps", tag="turned", bufs=BUFS["turned"])
            nc.tensor.transpose(out=vec_ps[:], in_=vec_rows[:], identity=ident_bf16[:])
            nc.vector.tensor_copy(
                out=cols[:].rearrange("p n j -> p (n j)"), in_=vec_ps[:, 0 : 5 * TILES]
            )
            nc.vector.tensor_add(out=tanh_bias[:], in0=cols[:, 1, :], in1=cols[:, 2, :])
            nc.vector.tensor_scalar_add(out=gate[:], in0=cols[:, 3, :], scalar1=TAU_EPS)
            nc.vector.reciprocal(out=gate[:], in_=gate[:])
            nc.vector.tensor_scalar(
                out=keep[:], in0=gate[:], scalar1=-1.0, scalar2=1.0, op0=ALU.mult, op1=ALU.add
            )

        def spread(column, dst, tag, factor):
            ps = psum.tile([P, TILES, P], F32, name="spread", tag=tag, bufs=BUFS[tag])
            for j in range(TILES):
                nc.tensor.transpose(
                    out=ps[:, j, :], in_=column[:, j : j + 1].to_broadcast([P, P]), identity=ident[:]
                )
            nc.scalar.mul(out=dst[:, 0:H], in_=ps[:].rearrange("p j m -> p (j m)"), mul=factor)

        st = [{} for g in range(GROUPS)]
        mean_var = kept.tile([P, GROUPS, HALF, 2], F32)
        rstd = kept.tile([P, GROUPS, HALF], F32)

        def words_turn(g, name):
            s = st[g]
            s[name + "T"] = stage.tile([P, GROUP, 2], F32, align_bytes=64, name="wordsT", bufs=5)
            tag = "turned" if g < 3 and (name == "liq" or EARLY_X) else "words"
            s["words"] = psum.tile([P, 2, 2, P], F32, name="words", tag=tag, bufs=BUFS[tag])
            turn_words(loaded[name, g], 0, s["words"])

        def words_copy(g, name):
            copy = nc.vector.tensor_copy if name == "liq" and g == 1 else nc.scalar.copy
            words_out(copy, st[g][name + "T"], 0, st[g]["words"])

        def quantise_stage(g, name):
            s = st[g]
            q = (
                codes.tile([P, GROUP], U32, align_bytes=64, name=name + "_words", bufs=6 if name == "x" else 3),
                codes.tile([P, GROUP], U8, align_bytes=64, name=name + "_scales", bufs=6 if name == "x" else 3),
            )
            s[name + "_q"] = (q[0][:], q[1][:])
            src = s["v_bf16"][:].rearrange("p n j -> p (n j)") if name == "v" else bf16_view(s[name + "T"])
            quantise(src, s[name + "_q"])

        def v_mx(g, t):
            s = st[g]
            s["v_acc", t] = psum.tile([P, TILES, P], F32, name="v_acc", tag="first", bufs=BUFS["first"])
            for j in range(TILES):
                mx_pass(s["v_acc", t][:, j, :], chunk(weights["v"], j), chunk(s["liq_q"], t))

        def v_out(g, t):
            s = st[g]
            if t == 0:
                s["v_bf16"] = stage.tile([P, GROUP, TILES], BF16, align_bytes=64, name="v_bf16")
            nc.vector.tensor_tensor(
                out=s["v_bf16"][:, t * P : (t + 1) * P, :],
                in0=s["v_acc", t][:].rearrange("p j n -> p n j"),
                in1=bv[:].unsqueeze(1).to_broadcast([P, P, TILES]),
                op=ALU.add,
            )

        def att_mx(g, i):
            s = st[g]
            s["att", i] = psum.tile([P, 2, GROUP], F32, name="att", tag="second", bufs=BUFS["second"])
            for jj in range(2):
                mx_pass(s["att", i][:, jj, :], chunk(weights["o"], 2 * i + jj), s["v_q"])

        def att_out(g, i):
            s = st[g]
            if i == 0:
                s["attT"] = work.tile([P, TILES, GROUP], F32, name="attT")
            for jj in range(2):
                j = 2 * i + jj
                if g < 2 and jj == 1:
                    nc.vector.tensor_scalar_add(
                        out=s["attT"][:, j, :], in0=s["att", i][:, jj, :], scalar1=cols[:, 0, j : j + 1]
                    )
                else:
                    nc.scalar.activation(
                        out=s["attT"][:, j, :], in_=s["att", i][:, jj, :], func=ACT.Identity, bias=cols[:, 0, j : j + 1]
                    )

        def u_open(g, t):
            s = st[g]
            s["u", t] = psum.tile([P, H], F32, name="u", tag="turned", bufs=BUFS["turned"])
            nc.tensor.matmul(out=s["u", t][:], lhsT=ident_bf16[:], rhs=loaded["liq", g][:, t, :], start=True, stop=False)

        def u_turn(g, t):
            s = st[g]
            for j in range(TILES):
                nc.tensor.matmul(
                    out=s["u", t][:, j * P : (j + 1) * P], lhsT=s["attT"][:, j, t * P : (t + 1) * P], rhs=ident[:],
                    is_transpose=True, start=False, stop=j == TILES - 1,
                )

        def bn_stage(g, t):
            s = st[g]
            s["stats", t] = small.tile([P, 6], F32, name="stats")
            nc.vector.bn_stats(out=s["stats", t][:], in_=s["u", t][:])

        def bn_end(g, t):
            nc.vector.bn_aggr(out=mean_var[:, g, t, :], in_=st[g]["stats", t][:])

        def rstd_stage(g0, g1):
            nc.gpsimd.tensor_scalar(
                out=rstd[:, g0:g1, :], in0=mean_var[:, g0:g1, :, 1], scalar1=1.0, scalar2=LN_EPS,
                op0=ALU.mult, op1=ALU.add,
            )
            nc.gpsimd.tensor_tensor(
                out=rstd[:, g0:g1, :], in0=rstd[:, g0:g1, :], in1=minus_half[:, 0 : g1 - g0, :], op=ALU.pow
            )

        def centre(g, t):
            s = st[g]
            if t == 0:
                s["w"] = kept.tile([P, HALF, W], F32, name="w%d" % g)
            nc.scalar.activation(
                out=s["w"][:, t, 0:H], in_=s["u", t][:], func=ACT.Identity, scale=-1.0, bias=mean_var[:, g, t, 0:1]
            )

        def gain_open(g):
            nc.vector.memset(st[g]["w"][:, :, H:W], 0.0)

        def gain_stage(g, t):
            w = st[g]["w"]
            nc.gpsimd.tensor_tensor(out=w[:, t, :], in0=w[:, t, :], in1=minus_g[:], op=ALU.mult)

        def xin_mx(g, t):
            s = st[g]
            s["xin", t] = psum.tile([P, H], F32, name="xin", tag="first", bufs=BUFS["first"])
            half = slice(0, H // 2)
            mx_pass(s["xin", t][:, half], chunk(s["x_q"], t), (weights["in"][0][:, half], weights["in"][1][:, half]))
            mx_pass(s["xin", t][:], chunk(s["x_q"], t), weights["in"])

        def s_stage(g, t):
            s = st[g]
            nc.vector.scalar_tensor_tensor(
                out=s["w"][:, t, 0:H], in0=s["w"][:, t, 0:H], scalar=rstd[:, g, t : t + 1],
                in1=s["xin", t][:], op0=ALU.mult, op1=ALU.add,
            )

        def s_turn(g, i):
            s = st[g]
            s["sT", i] = psum.tile([P, 2, HALF, P], F32, name="sT", tag="second", bufs=BUFS["second"])
            for jj in range(2):
                j = 2 * i + jj
                for t in range(HALF):
                    nc.tensor.transpose(
                        out=s["sT", i][:, jj, t, :], in_=s["w"][:, t, j * P : (j + 1) * P], identity=ident[:]
                    )

        def tanh_stage(g, i):
            s = st[g]
            s["tanhT", i] = work.tile([P, 2, GROUP], F32, name="tanhT")
            for jj in range(2):
                j = 2 * i + jj
                nc.scalar.activation(
                    out=s["tanhT", i][:, jj, :], in_=s["sT", i][:, jj, :, :].rearrange("p t n -> p (t n)"),
                    func=ACT.Tanh, bias=tanh_bias[:, j : j + 1],
                )

        def gate_stage(g, i):
            s = st[g]
            if i == 0:
                s["gatedT"] = work.tile([P, TILES, GROUP], F32, align_bytes=64, name="gatedT", tag="gatedT")
            for jj in range(2):
                j = 2 * i + jj
                if g >= LAST and jj == 1:
                    nc.vector.tensor_scalar_mul(
                        out=s["gatedT"][:, j, :], in0=s["tanhT", i][:, jj, :], scalar1=gate[:, j : j + 1]
                    )
                else:
                    nc.scalar.activation(
                        out=s["gatedT"][:, j, :], in_=s["tanhT", i][:, jj, :], func=ACT.Copy, scale=gate[:, j : j + 1]
                    )

        def keep_open(g):
            s = st[g]
            s["out"] = work.tile([P, HALF, H], F32, name="out", bufs=OUT)
            nc.vector.memset(s["out"][:, :, 0:1], 0.0)

        def keep_stage(g, t):
            s = st[g]
            nc.gpsimd.tensor_tensor(
                out=s["out"][:, t, :], in0=loaded["h", g][:, t, :], in1=keep_all[:], op=ALU.mult
            )

        def back_turn(g, t):
            s = st[g]
            s["back", t] = psum.tile([P, H], F32, name="back", tag="turned", bufs=BUFS["turned"])
            for j in range(TILES):
                nc.tensor.transpose(
                    out=s["back", t][:, j * P : (j + 1) * P], in_=s["gatedT"][:, j, t * P : (t + 1) * P],
                    identity=ident[:],
                )

        def out_stage(g, t):
            s = st[g]
            nc.vector.tensor_tensor(out=s["out"][:, t, :], in0=s["back", t][:], in1=s["out"][:, t, :], op=ALU.add)
            if g == GROUPS - 1:
                nc.sync.dma_start(out=group_rows(out, g)[:, t, :], in_=s["out"][:, t, :])
            elif t == HALF - 1:
                nc.sync.dma_start(out=group_rows(out, g), in_=s["out"][:])

        def both(stage_fn, g):
            if 0 <= g < GROUPS:
                for i in range(HALF):
                    stage_fn(g, i)

        def one(stage_fn, g, *args):
            if 0 <= g < GROUPS:
                stage_fn(g, *args)

        VG, AG, UG, WG, GG = 3, 4, 5, 6, 7
        XG = GROUPS + 1
        MG, TG, BG = XG + 3, XG + 4, XG + 6
        EARLY_X = 0
        WI = XG - 14
        keep_at = {3 + g if g < 3 else BG + g - 3: g for g in range(GROUPS)}
        x_at = {2 + g if g < 0 else XG + g: g for g in range(GROUPS)}
        for k in range(GROUPS + BG):
            load("liq", liq, k + 3)
            load("h", h, keep_at.get(k + 2, -1))
            load("x", x, x_at.get(k + 2, -1))
            if k > 2:
                one(quantise_stage, k - 2, "liq")
            if k - GG < GROUPS:
                one(quantise_stage, x_at.get(k - 2, -1), "x")
            one(gain_open, k - GG)
            one(quantise_stage, k - AG, "v")
            one(keep_open, keep_at.get(k, -1))
            if k - GG >= GROUPS:
                one(quantise_stage, x_at.get(k - 2, -1), "x")
            both(v_mx, k - VG)
            both(att_mx, k - AG)
            both(xin_mx, k - MG)
            one(u_open, k - UG, 0)
            one(words_turn, k, "liq")
            if k < 3:
                one(words_copy, k, "liq")
                if k == 0:
                    quantise_stage(0, "liq")
            if k == 1:
                weight_words("o", 0, "second", nc.vector.tensor_copy)
                weight_words("o", 1, "second", nc.scalar.copy)
            elif k == 2:
                vectors()
                weight_quantise("o")
            elif k == 3:
                spread(cols[:, 4, :], minus_g, "turned", -1.0)
                spread(keep, keep_all, "turned", 1.0)
            if k == WI:
                weight_words("in", 0, "turned", nc.scalar.copy)
            elif k == WI + 1:
                weight_words("in", 1, "turned", nc.scalar.copy)
            elif k == WI + 4:
                weight_quantise("in")
            both(bn_stage, k - WG)
            one(bn_end, k - WG, 0)
            one(centre, k - WG, 0)
            one(v_out, k - VG, 0)
            one(bn_end, k - WG, 1)
            one(centre, k - WG, 1)
            one(v_out, k - VG, 1)
            both(att_out, k - AG)
            if k >= 3:
                one(words_copy, k, "liq")
            both(s_stage, k - MG)
            one(u_turn, k - UG, 0)
            one(u_open, k - UG, 1)
            one(u_turn, k - UG, 1)
            both(back_turn, k - BG)
            one(words_turn, x_at.get(k, -1), "x")
            both(s_turn, k - TG)
            one(words_copy, x_at.get(k, -1), "x")
            both(tanh_stage, k - TG)
            both(out_stage, k - BG)
            both(gain_stage, k - GG)
            both(keep_stage, keep_at.get(k, -1))
            if k - WG in (7, 15):
                rstd_stage(k - WG - 7, k - WG + 1)
            both(gate_stage, k - TG)
